import numpy as np
import ml_dtypes


def mxq(x, axis, fmt="e4m3"):
    dtype, down = {"e4m3": (ml_dtypes.float8_e4m3fn, 7), "e5m2": (ml_dtypes.float8_e5m2, 14)}[fmt]
    v = np.moveaxis(np.asarray(x, np.float32).astype(ml_dtypes.bfloat16).astype(np.float64), axis, -1)
    blocks = v.reshape(v.shape[:-1] + (-1, 32))
    amax = np.abs(blocks).max(-1, keepdims=True)
    byte = np.maximum(np.where(amax > 0, np.frexp(amax)[1] - 1 + 127, 0) - down, 1)
    scale = np.exp2(byte - 127.0)
    codes = (blocks / scale).astype(np.float32).astype(dtype).astype(np.float64)
    return np.moveaxis((codes * scale).reshape(v.shape), -1, axis)


WIDE = False


def mx_kscale(k):
    if not WIDE:
        return np.ones(k)
    levels = np.array([10, -10, 5, -5, 0])
    a = np.random.permutation(np.resize(levels, k // 512 * 4)).reshape(k // 512, 4)
    idx = np.arange(k)
    return np.exp2(a[idx // 512, idx % 128 // 32])


BF16 = ml_dtypes.bfloat16


def bf(x):
    return np.asarray(x, np.float32).astype(BF16)


def f64(x):
    return np.asarray(x).astype(np.float64)


B, N, F, DIM, H, DH, D3 = 2, 24, 16, 1024, 12, 64, 512
W = H * D3
SCALE = 1.0 / (np.sqrt(DH) * H)
QS = np.sqrt(1.5 / (SCALE * np.sqrt(D3)))


def setup_inputs():
    s, t = mx_kscale(DIM), mx_kscale(D3)
    th = np.tile(t, H)
    return {"x": bf(np.random.standard_normal((B, N * F, DIM)) * s),
            "Wq": bf(np.random.standard_normal((DIM, W)) * QS / np.sqrt(DIM) / s[:, None] * th),
            "bq": bf(np.random.standard_normal(W) * 0.2 * QS * th),
            "k": bf(np.random.standard_normal((B, H, N, F, D3)) * QS / t)}


def reference(x, Wq, bq, k):
    y = (mxq(f64(x), 2, "e4m3") @ mxq(f64(Wq), 0, "e4m3")) + f64(bq)
    q = y.reshape(B, F, N, H, D3).transpose(0, 3, 2, 1, 4)
    s = (mxq(q, 4, "e4m3") @ mxq(f64(k), 4, "e4m3").transpose(0, 1, 2, 4, 3)) * SCALE
    e = np.exp(s - s.max(-1, keepdims=True))
    return e / e.sum(-1, keepdims=True)

@@ -1,0 +1,337 @@
+from contextlib import ExitStack
+
+import concourse.mybir as mybir
+from concourse.masks import make_identity
+
+F32 = mybir.dt.float32
+BF16 = mybir.dt.bfloat16
+U32 = mybir.dt.uint32
+U8 = mybir.dt.uint8
+FP8X4 = mybir.dt.float8_e4m3fn_x4
+ALU = mybir.AluOpType
+ACT = mybir.ActivationFunctionType
+AX = mybir.AxisListType
+
+P = 128
+HEADS = 12
+FLOPS = 2 * 768 * 1024 * 6144 + 2 * 576 * 16 * 16 * 512
+SCALE = 1.0 / 96.0
+BIG = 2.0 ** 100
+SG_TILES = ()
+G_PIECES = 0
+MANUAL = True
+BATCHES = ((0, 4), (4, 8), (8, 11), (11, 12))
+
+
+def tile_dividedspacetimeattention_pa_kernel(tc, x, Wq, bq, k, out):
+    nc = tc.nc
+    with ExitStack() as ctx:
+        consts = ctx.enter_context(tc.tile_pool(name="consts", bufs=1))
+        wraw_p = ctx.enter_context(tc.tile_pool(name="wraw", bufs=4))
+        kraw_p = ctx.enter_context(tc.tile_pool(name="kraw", bufs=3))
+        wg_p = ctx.enter_context(tc.tile_pool(name="wg", bufs=3))
+        wq_p = ctx.enter_context(tc.tile_pool(name="wq", bufs=2))
+        kg_p = ctx.enter_context(tc.tile_pool(name="kg", bufs=2))
+        kq_p = ctx.enter_context(tc.tile_pool(name="kq", bufs=2))
+        qg_p = ctx.enter_context(tc.tile_pool(name="qg", bufs=2))
+        qq_p = ctx.enter_context(tc.tile_pool(name="qq", bufs=2))
+        yf_p = ctx.enter_context(tc.tile_pool(name="yf", bufs=2))
+        sm_p = ctx.enter_context(tc.tile_pool(name="sm", bufs=2))
+        ps_y = ctx.enter_context(tc.psum_pool(name="psy", bufs=3))
+        ps_t = ctx.enter_context(tc.psum_pool(name="pst", bufs=3))
+        ps_s = ctx.enter_context(tc.psum_pool(name="pss", bufs=2))
+        if MANUAL:
+            ctx.enter_context(tc.manual_schedule())
+
+        wraw, kraw, wgs, wcs, kgs, kcs, qgs, qcs, scs, zts = {}, {}, {}, {}, {}, {}, {}, {}, {}, {}
+
+        def copy_on(eng, dst, src):
+            if eng == "v":
+                nc.vector.tensor_copy(out=dst, in_=src)
+            elif eng == "s":
+                nc.scalar.copy(out=dst, in_=src)
+            else:
+                nc.gpsimd.tensor_scalar(out=dst, in0=src, scalar1=1.0, scalar2=0.0, op0=ALU.mult, op1=ALU.add)
+
+        def quant(src, codes, scales, lo, width):
+            nc.vector.quantize_mx(
+                out=codes[:, lo // 4:(lo + width) // 4].bitcast(FP8X4),
+                scales=scales[:, lo // 4:(lo + width) // 4],
+                in_=src[:, lo:lo + width],
+            )
+
+        def mx(dst, a, a_s, a0, b, b_s, b0, start, stop):
+            nc.tensor.matmul_mx(
+                out=dst,
+                lhsT=a[:, a0:a0 + P].bitcast(FP8X4),
+                lhsT_scale=a_s[:, a0:a0 + P],
+                rhs=b[:, b0:b0 + P].bitcast(FP8X4),
+                rhs_scale=b_s[:, b0:b0 + P],
+                start=start,
+                stop=stop,
+            )
+
+        def load_w(h):
+            w_raw = wraw_p.tile([P, 4096], BF16)
+            wv = w_raw[:].rearrange("p (c j w) -> p c j w", c=2, j=4)
+            for c in range(2):
+                for u in range(2):
+                    r0 = 512 * c + 256 * u
+                    nc.sync.dma_start(
+                        out=wv[:, c, 2 * u:2 * u + 2, :],
+                        in_=Wq[r0:r0 + 256, h * 512:(h + 1) * 512].rearrange("(p e) w -> p e w", e=2),
+                    )
+            wraw[h] = w_raw
+
+        k_rows = k.rearrange("b h n g d -> b h (n g) d")
+
+        def load_k(h):
+            k_raw = kraw_p.tile([P, 3072], BF16)
+            kv = k_raw[:].rearrange("p (i d) -> p i d", i=6)
+            for b in range(2):
+                nc.sync.dma_start(
+                    out=kv[:, 3 * b:3 * b + 3, :],
+                    in_=k_rows[b, h].rearrange("(s p) d -> p s d", s=3),
+                )
+            kraw[h] = k_raw
+
+        ident = consts.tile([P, P], F32)
+        make_identity(nc, ident[:])
+        warm = consts.tile([P, 2], F32)
+        nc.vector.memset(warm[:], 0.0)
+        nc.scalar.activation(out=warm[:, 1:2], in_=warm[:, 0:1], func=ACT.Exp)
+        b_raw = consts.tile([P, 256], BF16)
+        nc.vector.memset(b_raw[:], 0.0)
+        mask_in = consts.tile([P, 1024], BF16, align_bytes=64)
+        nc.vector.memset(mask_in[:], 0.0)
+
+        x_raw = consts.tile([P, 6144], BF16)
+        xr_v = x_raw[:].rearrange("p (b r c) -> p b r c", b=2, r=3)
+
+        def load_x(b):
+            nc.sync.dma_start(out=xr_v[:, b], in_=x[b].rearrange("(p r) c -> p r c", r=3))
+
+        load_x(0)
+        nc.sync.dma_start(out=b_raw[0:24, :], in_=bq.rearrange("(r c) -> r c", c=256))
+        load_w(0)
+        load_x(1)
+        load_w(1)
+        load_k(0)
+        load_w(2)
+        load_k(1)
+        load_w(3)
+        load_k(2)
+
+        mv = mask_in[:].rearrange("p (o a f j) -> p o a f j", o=2, a=8, f=16)
+        eye8 = ident[:, 0:8].unsqueeze(2).to_broadcast([P, 8, 16])
+        nc.vector.tensor_copy(out=mv[:, 0, :, :, 0], in_=eye8)
+        nc.vector.tensor_scalar(out=mv[:, 1, :, :, 0], in0=eye8, scalar1=-1.0, scalar2=BIG, op0=ALU.add, op1=ALU.mult)
+        mask_c = consts.tile([P, 256], U32, align_bytes=64)
+        mask_s = consts.tile([P, 256], U8, align_bytes=64)
+        quant(mask_in, mask_c, mask_s, 0, 1024)
+
+        bt = ps_t.tile([P, 512], F32, tag="t")
+        nc.tensor.transpose(bt[:, 0:P], b_raw[:].bitcast(F32), ident[:])
+        bias = consts.tile([P, 48], F32)
+        nc.vector.tensor_copy(out=bias[:], in_=bt[:, 0:24].bitcast(BF16))
+
+        xw = x_raw[:].bitcast(F32).rearrange("p (b r w) -> p b r w", b=2, r=3)
+        xg = consts.tile([P, 6144], BF16, align_bytes=64)
+        xg_w = xg[:].bitcast(F32).rearrange("p (c n f u) -> p c n f u", c=2, n=48, f=16)
+        xc = consts.tile([P, 1536], U32, align_bytes=64)
+        xs = consts.tile([P, 1536], U8, align_bytes=64)
+
+        def prep_x(b):
+            for r in range(3):
+                xt = ps_t.tile([P, 512], F32, tag="t")
+                xt_v = xt[:].rearrange("p (q t) -> p q t", q=4)
+                for q in range(4):
+                    nc.tensor.transpose(xt_v[:, q, :], xw[:, b, r, q * P:(q + 1) * P], ident[:])
+                for c in range(2):
+                    copy_on(
+                        "v" if c == 0 else "s",
+                        xg_w[:, c, b * 24 + r:(b + 1) * 24:3, :, :],
+                        xt_v[:, 2 * c:2 * c + 2, :].rearrange("p u (f a) -> p a f u", a=8),
+                    )
+
+        def quant_x(b):
+            for c in range(2):
+                quant(xg, xc, xs, c * 3072 + b * 1536, 1024)
+                quant(xg, xc, xs, c * 3072 + b * 1536 + 1024, 512)
+
+        def regroup(h, engines):
+            wg = wg_p.tile([P, 4096], BF16, align_bytes=64)
+            dst = wg[:].rearrange("p (c e q i j) -> p c e q j i", c=2, e=2, q=64, i=4, j=4)
+            src = wraw[h][:].rearrange("p (c j q i e) -> p c e q j i", c=2, j=4, q=64, i=4, e=2)
+            for n in range(4):
+                copy_on(engines[n], dst[:, n // 2, n % 2], src[:, n // 2, n % 2])
+            wgs[h] = wg
+
+        def quant_w(h):
+            wc = wq_p.tile([P, 1024], U32, align_bytes=64)
+            ws = wq_p.tile([P, 1024], U8, align_bytes=64)
+            quant(wgs[h], wc, ws, 0, 4096)
+            wcs[h] = (wc, ws)
+
+        def prep_k(h):
+            kw = kraw[h][:].bitcast(F32).rearrange("p (i w) -> p i w", i=6)
+            kg = kg_p.tile([P, 3072], BF16, align_bytes=64)
+            kg_w = kg[:].bitcast(F32).rearrange("p (i r u) -> p i r u", i=6, u=2)
+            kts = []
+            for jj in range(3):
+                kt = ps_t.tile([P, 512], F32, tag="t")
+                kt_v = kt[:].rearrange("p (i u r) -> p i u r", i=2, u=2)
+                for ii in range(2):
+                    for u in range(2):
+                        nc.tensor.transpose(kt_v[:, ii, u, :], kw[:, 2 * jj + ii, u * P:(u + 1) * P], ident[:])
+                kts.append(kt_v)
+            for jj in range(3):
+                nc.scalar.copy(out=kg_w[:, 2 * jj:2 * jj + 2], in_=kts[jj].rearrange("p i u r -> p i r u"))
+            kgs[h] = kg
+
+        def quant_k(h):
+            kc = kq_p.tile([P, 768], U32, align_bytes=64)
+            ks = kq_p.tile([P, 768], U8, align_bytes=64)
+            quant(kgs[h], kc, ks, 0, 2048)
+            quant(kgs[h], kc, ks, 2048, 1024)
+            kcs[h] = (kc, ks)
+
+        def main(h, i):
+            wc, ws = wcs[h]
+            y = ps_y.tile([P, 512], F32, tag="y")
+            yv = y[:].rearrange("p (j r) -> p j r", j=4)
+            for j in range(4):
+                tau = 2 * (j % 2) + j // 2
+                for c in range(2):
+                    mx(yv[:, j, :], wc, ws, c * 512 + tau * P, xc, xs, c * 768 + i * P, c == 0, c == 1)
+            y_rj = y[:].rearrange("p (j r) -> p r j", j=4)
+            q_rj = qgs[h][:, i * 512:(i + 1) * 512].rearrange("p (r j) -> p r j", j=4)
+            b_rj = bias[:, h * 4:(h + 1) * 4].unsqueeze(1).to_broadcast([P, P, 4])
+            if i in SG_TILES:
+                yf = yf_p.tile([P, 512], F32)
+                yf_rj = yf[:].rearrange("p (r j) -> p r j", j=4)
+                nc.scalar.copy(out=yf_rj, in_=y_rj)
+                nc.gpsimd.tensor_tensor(out=q_rj, in0=yf_rj, in1=b_rj, op=ALU.add)
+            else:
+                nc.vector.tensor_tensor(out=q_rj, in0=y_rj, in1=b_rj, op=ALU.add)
+
+        def quant_q(h):
+            qc = qq_p.tile([P, 768], U32, align_bytes=64)
+            qs = qq_p.tile([P, 768], U8, align_bytes=64)
+            quant(qgs[h], qc, qs, 0, 2048)
+            quant(qgs[h], qc, qs, 2048, 1024)
+            qcs[h] = (qc, qs)
+
+        def batch_of(h):
+            for n in range(len(BATCHES)):
+                if BATCHES[n][0] <= h < BATCHES[n][1]:
+                    return n
+            return -1
+
+        def scores(h):
+            qc, qs = qcs[h]
+            kc, ks = kcs[h]
+            n = batch_of(h)
+            h0, h1 = BATCHES[n]
+            if h == h0:
+                zt = sm_p.tile([P, 384], F32)
+                zts[n] = zt
+            zv = zts[n][:, 0:(h1 - h0) * 96].rearrange("p (b t g) -> p b t g", b=2, g=16)
+            tiles = []
+            for b in range(2):
+                sc = ps_s.tile([P, 384], F32, tag="s")
+                sc_v = sc[:].rearrange("p (s c) -> p s c", s=3)
+                for s in range(3):
+                    i = 3 * b + s
+                    mx(sc_v[:, s, :], qc, qs, i * P, kc, ks, i * P, True, False)
+                    mx(sc_v[:, s, :], mask_c, mask_s, 0, mask_c, mask_s, P, False, True)
+                tiles.append(sc)
+            for b in range(2):
+                nc.vector.tensor_reduce(
+                    out=zv[:, b, (h - h0) * 3:(h - h0 + 1) * 3, :],
+                    in_=tiles[b][:].rearrange("p (s a g) -> p s g a", s=3, a=8),
+                    axis=AX.X,
+                    op=ALU.max,
+                )
+
+        out_v = out.rearrange("b h (s a) f g -> b (h s) (a f) g", s=3)
+        soft = {}
+
+        def softmax_a(n, last):
+            h0, h1 = BATCHES[n]
+            groups = (h1 - h0) * 6
+            zg = zts[n][:, 0:groups * 16].rearrange("p (t g) -> p t g", g=16)
+            mxs = sm_p.tile([P, 24], F32)
+            nc.vector.tensor_reduce(out=mxs[:, 0:groups], in_=zg, axis=AX.X, op=ALU.max)
+            eng = nc.vector if last else nc.gpsimd
+            eng.tensor_tensor(out=zg, in0=zg, in1=mxs[:, 0:groups].unsqueeze(2).to_broadcast([P, groups, 16]), op=ALU.subtract)
+            ex = sm_p.tile([P, 384], F32)
+            nc.scalar.activation(out=ex[:, 0:groups * 16], in_=zts[n][:, 0:groups * 16], func=ACT.Exp, scale=SCALE)
+            soft[n] = ex
+
+        def softmax_b(n, last):
+            h0, h1 = BATCHES[n]
+            groups = (h1 - h0) * 6
+            ex = soft[n]
+            eg = ex[:, 0:groups * 16].rearrange("p (t g) -> p t g", g=16)
+            sums = sm_p.tile([P, 24], F32)
+            nc.vector.tensor_reduce(out=sums[:, 0:groups], in_=eg, axis=AX.X, op=ALU.add)
+            rec = sm_p.tile([P, 24], F32)
+            nc.vector.reciprocal(out=rec[:, 0:groups], in_=sums[:, 0:groups])
+            eng = nc.vector if last else nc.gpsimd
+            eng.tensor_tensor(out=eg, in0=eg, in1=rec[:, 0:groups].unsqueeze(2).to_broadcast([P, groups, 16]), op=ALU.mult)
+            eb = ex[:, 0:groups * 16].rearrange("p (b t g) -> p b t g", b=2, g=16)
+            for b in range(2):
+                nc.sync.dma_start(out=out_v[b, h0 * 3:h1 * 3].rearrange("t p g -> p t g"), in_=eb[:, b])
+
+        steady = ["g"] * G_PIECES + ["s"] * (4 - G_PIECES)
+        prep_x(0)
+        regroup(0, ["v", "s", "v", "s"])
+        quant_x(0)
+        quant_w(0)
+        prep_x(1)
+        quant_x(1)
+        regroup(1, ["s", "g", "s", "g"])
+
+        for h in range(HEADS):
+            qg = qg_p.tile([P, 3072], BF16, align_bytes=64)
+            qgs[h] = qg
+            if h + 4 < HEADS:
+                load_w(h + 4)
+            main(h, 0)
+            main(h, 1)
+            main(h, 2)
+            done = -1
+            if h > 0:
+                scores(h - 1)
+                n = batch_of(h - 1)
+                if BATCHES[n][1] == h:
+                    done = n
+                    softmax_a(n, False)
+            if h > 0:
+                prep_k(h)
+                if h + 3 < HEADS:
+                    load_k(h + 3)
+            main(h, 3)
+            if 1 <= h < HEADS - 1:
+                quant_w(h + 1)
+            main(h, 4)
+            if done >= 0:
+                softmax_b(done, False)
+            main(h, 5)
+            if h == 0:
+                prep_k(0)
+                load_k(3)
+            if h + 2 < HEADS:
+                regroup(h + 2, steady)
+            if h == 0:
+                quant_q(0)
+                quant_w(1)
+                quant_k(0)
+            else:
+                quant_k(h)
+                quant_q(h)
+
+        scores(HEADS - 1)
+        softmax_a(len(BATCHES) - 1, True)
+        softmax_b(len(BATCHES) - 1, True)

@@ -14,13 +14,13 @@ AX = mybir.AxisListType
 
 P = 128
 HEADS = 12
+LAST = HEADS - 1
 FLOPS = 2 * 768 * 1024 * 6144 + 2 * 576 * 16 * 16 * 512
 SCALE = 1.0 / 96.0
 BIG = 2.0 ** 100
-SG_TILES = ()
-G_PIECES = 0
-MANUAL = True
-BATCHES = ((0, 4), (4, 8), (8, 11), (11, 12))
+SG_TILES = (0, 1)
+STEADY = ("s", "s", "s", "g")
+BATCHES = ((0, 4), (4, 8), (8, 11))
 
 
 def tile_dividedspacetimeattention_pa_kernel(tc, x, Wq, bq, k, out):
@@ -40,10 +40,9 @@ def tile_dividedspacetimeattention_pa_kernel(tc, x, Wq, bq, k, out):
         ps_y = ctx.enter_context(tc.psum_pool(name="psy", bufs=3))
         ps_t = ctx.enter_context(tc.psum_pool(name="pst", bufs=3))
         ps_s = ctx.enter_context(tc.psum_pool(name="pss", bufs=2))
-        if MANUAL:
-            ctx.enter_context(tc.manual_schedule())
+        ctx.enter_context(tc.manual_schedule())
 
-        wraw, kraw, wgs, wcs, kgs, kcs, qgs, qcs, scs, zts = {}, {}, {}, {}, {}, {}, {}, {}, {}, {}
+        wraw, kraw, wgs, wcs, kgs, kcs, qgs, qcs, ys, kts, scs = {}, {}, {}, {}, {}, {}, {}, {}, {}, {}, {}
 
         def copy_on(eng, dst, src):
             if eng == "v":
@@ -116,11 +115,10 @@ def tile_dividedspacetimeattention_pa_kernel(tc, x, Wq, bq, k, out):
         load_w(0)
         load_x(1)
         load_w(1)
-        load_k(0)
         load_w(2)
-        load_k(1)
+        load_k(0)
         load_w(3)
-        load_k(2)
+        load_k(1)
 
         mv = mask_in[:].rearrange("p (o a f j) -> p o a f j", o=2, a=8, f=16)
         eye8 = ident[:, 0:8].unsqueeze(2).to_broadcast([P, 8, 16])
@@ -173,20 +171,22 @@ def tile_dividedspacetimeattention_pa_kernel(tc, x, Wq, bq, k, out):
             quant(wgs[h], wc, ws, 0, 4096)
             wcs[h] = (wc, ws)
 
-        def prep_k(h):
+        def k_transposes(h):
             kw = kraw[h][:].bitcast(F32).rearrange("p (i w) -> p i w", i=6)
-            kg = kg_p.tile([P, 3072], BF16, align_bytes=64)
-            kg_w = kg[:].bitcast(F32).rearrange("p (i r u) -> p i r u", i=6, u=2)
-            kts = []
+            kts[h] = []
             for jj in range(3):
                 kt = ps_t.tile([P, 512], F32, tag="t")
                 kt_v = kt[:].rearrange("p (i u r) -> p i u r", i=2, u=2)
                 for ii in range(2):
                     for u in range(2):
                         nc.tensor.transpose(kt_v[:, ii, u, :], kw[:, 2 * jj + ii, u * P:(u + 1) * P], ident[:])
-                kts.append(kt_v)
+                kts[h].append(kt_v)
+
+        def k_evac(h):
+            kg = kg_p.tile([P, 3072], BF16, align_bytes=64)
+            kg_w = kg[:].bitcast(F32).rearrange("p (i r u) -> p i r u", i=6, u=2)
             for jj in range(3):
-                nc.scalar.copy(out=kg_w[:, 2 * jj:2 * jj + 2], in_=kts[jj].rearrange("p i u r -> p i r u"))
+                nc.scalar.copy(out=kg_w[:, 2 * jj:2 * jj + 2], in_=kts[h][jj].rearrange("p i u r -> p i r u"))
             kgs[h] = kg
 
         def quant_k(h):
@@ -196,7 +196,7 @@ def tile_dividedspacetimeattention_pa_kernel(tc, x, Wq, bq, k, out):
             quant(kgs[h], kc, ks, 2048, 1024)
             kcs[h] = (kc, ks)
 
-        def main(h, i):
+        def mm(h, i):
             wc, ws = wcs[h]
             y = ps_y.tile([P, 512], F32, tag="y")
             yv = y[:].rearrange("p (j r) -> p j r", j=4)
@@ -204,10 +204,13 @@ def tile_dividedspacetimeattention_pa_kernel(tc, x, Wq, bq, k, out):
                 tau = 2 * (j % 2) + j // 2
                 for c in range(2):
                     mx(yv[:, j, :], wc, ws, c * 512 + tau * P, xc, xs, c * 768 + i * P, c == 0, c == 1)
-            y_rj = y[:].rearrange("p (j r) -> p r j", j=4)
+            ys[(h, i)] = y
+
+        def ev(h, i, through_gpsimd):
+            y_rj = ys[(h, i)][:].rearrange("p (j r) -> p r j", j=4)
             q_rj = qgs[h][:, i * 512:(i + 1) * 512].rearrange("p (r j) -> p r j", j=4)
             b_rj = bias[:, h * 4:(h + 1) * 4].unsqueeze(1).to_broadcast([P, P, 4])
-            if i in SG_TILES:
+            if through_gpsimd:
                 yf = yf_p.tile([P, 512], F32)
                 yf_rj = yf[:].rearrange("p (r j) -> p r j", j=4)
                 nc.scalar.copy(out=yf_rj, in_=y_rj)
@@ -215,123 +218,133 @@ def tile_dividedspacetimeattention_pa_kernel(tc, x, Wq, bq, k, out):
             else:
                 nc.vector.tensor_tensor(out=q_rj, in0=y_rj, in1=b_rj, op=ALU.add)
 
-        def quant_q(h):
+        def new_q(h):
+            qg = qg_p.tile([P, 3072], BF16, align_bytes=64)
             qc = qq_p.tile([P, 768], U32, align_bytes=64)
             qs = qq_p.tile([P, 768], U8, align_bytes=64)
-            quant(qgs[h], qc, qs, 0, 2048)
-            quant(qgs[h], qc, qs, 2048, 1024)
+            qgs[h] = qg
             qcs[h] = (qc, qs)
 
-        def batch_of(h):
-            for n in range(len(BATCHES)):
-                if BATCHES[n][0] <= h < BATCHES[n][1]:
-                    return n
-            return -1
+        def quant_q(h, lo, width):
+            quant(qgs[h], qcs[h][0], qcs[h][1], lo, width)
 
-        def scores(h):
+        def s2(h, b):
             qc, qs = qcs[h]
             kc, ks = kcs[h]
-            n = batch_of(h)
-            h0, h1 = BATCHES[n]
-            if h == h0:
-                zt = sm_p.tile([P, 384], F32)
-                zts[n] = zt
-            zv = zts[n][:, 0:(h1 - h0) * 96].rearrange("p (b t g) -> p b t g", b=2, g=16)
-            tiles = []
-            for b in range(2):
-                sc = ps_s.tile([P, 384], F32, tag="s")
-                sc_v = sc[:].rearrange("p (s c) -> p s c", s=3)
-                for s in range(3):
-                    i = 3 * b + s
-                    mx(sc_v[:, s, :], qc, qs, i * P, kc, ks, i * P, True, False)
-                    mx(sc_v[:, s, :], mask_c, mask_s, 0, mask_c, mask_s, P, False, True)
-                tiles.append(sc)
-            for b in range(2):
-                nc.vector.tensor_reduce(
-                    out=zv[:, b, (h - h0) * 3:(h - h0 + 1) * 3, :],
-                    in_=tiles[b][:].rearrange("p (s a g) -> p s g a", s=3, a=8),
-                    axis=AX.X,
-                    op=ALU.max,
-                )
+            sc = ps_s.tile([P, 384], F32, tag="s")
+            sc_v = sc[:].rearrange("p (s c) -> p s c", s=3)
+            for s in range(3):
+                i = 3 * b + s
+                mx(sc_v[:, s, :], qc, qs, i * P, kc, ks, i * P, True, False)
+                mx(sc_v[:, s, :], mask_c, mask_s, 0, mask_c, mask_s, P, False, True)
+            scs[(h, b)] = sc
+
+        def ex(h, b, dst):
+            nc.vector.tensor_reduce(
+                out=dst,
+                in_=scs[(h, b)][:].rearrange("p (s a g) -> p s g a", s=3, a=8),
+                axis=AX.X,
+                op=ALU.max,
+            )
 
         out_v = out.rearrange("b h (s a) f g -> b (h s) (a f) g", s=3)
-        soft = {}
 
-        def softmax_a(n, last):
-            h0, h1 = BATCHES[n]
-            groups = (h1 - h0) * 6
-            zg = zts[n][:, 0:groups * 16].rearrange("p (t g) -> p t g", g=16)
+        def softmax_a(z, e, groups, eng):
+            zg = z.rearrange("p (t g) -> p t g", g=16)
             mxs = sm_p.tile([P, 24], F32)
             nc.vector.tensor_reduce(out=mxs[:, 0:groups], in_=zg, axis=AX.X, op=ALU.max)
-            eng = nc.vector if last else nc.gpsimd
             eng.tensor_tensor(out=zg, in0=zg, in1=mxs[:, 0:groups].unsqueeze(2).to_broadcast([P, groups, 16]), op=ALU.subtract)
-            ex = sm_p.tile([P, 384], F32)
-            nc.scalar.activation(out=ex[:, 0:groups * 16], in_=zts[n][:, 0:groups * 16], func=ACT.Exp, scale=SCALE)
-            soft[n] = ex
+            nc.scalar.activation(out=e, in_=z, func=ACT.Exp, scale=SCALE)
 
-        def softmax_b(n, last):
-            h0, h1 = BATCHES[n]
-            groups = (h1 - h0) * 6
-            ex = soft[n]
-            eg = ex[:, 0:groups * 16].rearrange("p (t g) -> p t g", g=16)
+        def softmax_b(e, groups, eng):
+            eg = e.rearrange("p (t g) -> p t g", g=16)
             sums = sm_p.tile([P, 24], F32)
             nc.vector.tensor_reduce(out=sums[:, 0:groups], in_=eg, axis=AX.X, op=ALU.add)
             rec = sm_p.tile([P, 24], F32)
             nc.vector.reciprocal(out=rec[:, 0:groups], in_=sums[:, 0:groups])
-            eng = nc.vector if last else nc.gpsimd
             eng.tensor_tensor(out=eg, in0=eg, in1=rec[:, 0:groups].unsqueeze(2).to_broadcast([P, groups, 16]), op=ALU.mult)
-            eb = ex[:, 0:groups * 16].rearrange("p (b t g) -> p b t g", b=2, g=16)
-            for b in range(2):
-                nc.sync.dma_start(out=out_v[b, h0 * 3:h1 * 3].rearrange("t p g -> p t g"), in_=eb[:, b])
 
-        steady = ["g"] * G_PIECES + ["s"] * (4 - G_PIECES)
+        def store(e, b, h0, h1):
+            nc.sync.dma_start(out=out_v[b, h0 * 3:h1 * 3].rearrange("t p g -> p t g"), in_=e.rearrange("p (t g) -> p t g", g=16))
+
         prep_x(0)
-        regroup(0, ["v", "s", "v", "s"])
+        regroup(0, ["v", "s", "v", "g"])
         quant_x(0)
         quant_w(0)
         prep_x(1)
         quant_x(1)
         regroup(1, ["s", "g", "s", "g"])
 
+        zt, et, batch = None, None, None
         for h in range(HEADS):
-            qg = qg_p.tile([P, 3072], BF16, align_bytes=64)
-            qgs[h] = qg
+            new_q(h)
             if h + 4 < HEADS:
                 load_w(h + 4)
-            main(h, 0)
-            main(h, 1)
-            main(h, 2)
-            done = -1
-            if h > 0:
-                scores(h - 1)
-                n = batch_of(h - 1)
-                if BATCHES[n][1] == h:
-                    done = n
-                    softmax_a(n, False)
-            if h > 0:
-                prep_k(h)
-                if h + 3 < HEADS:
-                    load_k(h + 3)
-            main(h, 3)
-            if 1 <= h < HEADS - 1:
-                quant_w(h + 1)
-            main(h, 4)
-            if done >= 0:
-                softmax_b(done, False)
-            main(h, 5)
-            if h == 0:
-                prep_k(0)
-                load_k(3)
             if h + 2 < HEADS:
-                regroup(h + 2, steady)
-            if h == 0:
-                quant_q(0)
-                quant_w(1)
-                quant_k(0)
+                load_k(h + 2)
+            for i in range(2):
+                mm(h, i)
+                ev(h, i, h > 0 and i in SG_TILES)
+            if h + 2 < HEADS:
+                regroup(h + 2, STEADY if h > 0 else ["s", "g", "s", "g"])
+            mm(h, 2)
+            ev(h, 2, h > 0 and 2 in SG_TILES)
+            finished = None
+            if h > 0:
+                for bt_ in BATCHES:
+                    if bt_[0] == h - 1:
+                        batch = bt_
+                        zt = sm_p.tile([P, 384], F32)
+                        et = sm_p.tile([P, 384], F32)
+                width = (batch[1] - batch[0]) * 48
+                s2(h - 1, 0)
+                s2(h - 1, 1)
+                for b in range(2):
+                    lo = b * width + (h - 1 - batch[0]) * 48
+                    ex(h - 1, b, zt[:, lo:lo + 48].rearrange("p (t g) -> p t g", g=16))
+                if batch[1] == h:
+                    finished = batch
+                    softmax_a(zt[:, 0:2 * width], et[:, 0:2 * width], width // 8, nc.gpsimd)
+            mm(h, 3)
+            ev(h, 3, False)
+            if h > 0:
+                k_transposes(h)
+                k_evac(h)
+            if h < LAST:
+                quant_w(h + 1)
             else:
+                quant_q(h, 0, 1024)
+            mm(h, 4)
+            ev(h, 4, False)
+            if finished is not None:
+                width = (finished[1] - finished[0]) * 48
+                softmax_b(et[:, 0:2 * width], width // 8, nc.gpsimd)
+                for b in range(2):
+                    store(et[:, b * width:(b + 1) * width], b, finished[0], finished[1])
+            if h == LAST:
+                quant_q(h, 1024, 1024)
                 quant_k(h)
-                quant_q(h)
+            mm(h, 5)
+            ev(h, 5, False)
+            if h == 0:
+                k_transposes(0)
+                k_evac(0)
+            if h < LAST:
+                quant_q(h, 0, 2048)
+                quant_k(h)
+                quant_q(h, 2048, 1024)
 
-        scores(HEADS - 1)
-        softmax_a(len(BATCHES) - 1, True)
-        softmax_b(len(BATCHES) - 1, True)
+        zl = sm_p.tile([P, 96], F32)
+        el = sm_p.tile([P, 96], F32)
+        quant_q(LAST, 2048, 512)
+        s2(LAST, 0)
+        quant_q(LAST, 2560, 512)
+        ex(LAST, 0, zl[:, 0:48].rearrange("p (t g) -> p t g", g=16))
+        s2(LAST, 1)
+        softmax_a(zl[:, 0:48], el[:, 0:48], 3, nc.vector)
+        ex(LAST, 1, zl[:, 48:96].rearrange("p (t g) -> p t g", g=16))
+        softmax_a(zl[:, 48:96], el[:, 48:96], 3, nc.vector)
+        softmax_b(el[:, 0:48], 3, nc.vector)
+        store(el[:, 0:48], 0, LAST, HEADS)
+        softmax_b(el[:, 48:96], 3, nc.vector)
+        store(el[:, 48:96], 1, LAST, HEADS)

@@ -18,9 +18,106 @@ LAST = HEADS - 1
 FLOPS = 2 * 768 * 1024 * 6144 + 2 * 576 * 16 * 16 * 512
 SCALE = 1.0 / 96.0
 BIG = 2.0 ** 100
+BATCHES = ((0, 4), (4, 8), (8, 11), (11, 12))
+REGROUP_ENGINES = {0: "vsvs", 1: "sssg", 2: "sgsg"}
+REGROUP_DEFAULT = "sssg"
+SG_FIRST = ()
 SG_TILES = (0, 1)
-STEADY = ("s", "s", "s", "g")
-BATCHES = ((0, 4), (4, 8), (8, 11))
+SG_LAST = (0, 1)
+STEADY_STEPS = (
+    ("lw", 4),
+    ("lk", 2),
+    ("mm", 0, 0),
+    ("e", 0, 0),
+    ("mm", 0, 1),
+    ("e", 0, 1),
+    ("sm", 4),
+    ("sm", 5),
+    ("rg", 2),
+    ("mm", 0, 2),
+    ("e", 0, 2),
+    ("s2", -1),
+    ("ex", -1, 0),
+    ("ex", -1, 1),
+    ("sm", 1),
+    ("sm", 2),
+    ("mm", 0, 3),
+    ("e", 0, 3),
+    ("kt", 0),
+    ("ke", 0),
+    ("sm", 3),
+    ("qw", 1),
+    ("mm", 0, 4),
+    ("e", 0, 4),
+    ("mm", 0, 5),
+    ("e", 0, 5),
+    ("qqa", 0),
+    ("qk", 0),
+    ("qqb", 0),
+)
+FIRST_STEPS = (
+    ("lw", 4),
+    ("lk", 2),
+    ("mm", 0, 0),
+    ("e", 0, 0),
+    ("mm", 0, 1),
+    ("e", 0, 1),
+    ("rg", 2),
+    ("mm", 0, 2),
+    ("e", 0, 2),
+    ("mm", 0, 3),
+    ("e", 0, 3),
+    ("qw", 1),
+    ("mm", 0, 4),
+    ("e", 0, 4),
+    ("mm", 0, 5),
+    ("e", 0, 5),
+    ("kt", 0),
+    ("ke", 0),
+    ("qqa", 0),
+    ("qqb", 0),
+    ("qk", 0),
+)
+LAST_STEPS = (
+    ("mm", 0, 0),
+    ("e", 0, 0),
+    ("mm", 0, 1),
+    ("e", 0, 1),
+    ("sm", 4),
+    ("sm", 5),
+    ("mm", 0, 2),
+    ("e", 0, 2),
+    ("s2", -1),
+    ("ex", -1, 0),
+    ("ex", -1, 1),
+    ("sm", 1),
+    ("sm", 2),
+    ("mm", 0, 3),
+    ("e", 0, 3),
+    ("kt", 0),
+    ("ke", 0),
+    ("sm", 3),
+    ("qq", 0, 0, 1024),
+    ("mm", 0, 4),
+    ("e", 0, 4),
+    ("qq", 0, 1024, 1024),
+    ("sm", 4),
+    ("sm", 5),
+    ("mm", 0, 5),
+    ("e", 0, 5),
+    ("qk", 0),
+    ("qq", 0, 2048, 512),
+    ("s2b", 0, 0),
+    ("qq", 0, 2560, 512),
+    ("ex", 0, 0),
+    ("s2b", 0, 1),
+    ("ex", 0, 1),
+    ("sm", 1),
+    ("sm", 2),
+    ("sm", 3),
+    ("sm", 4),
+    ("sm", 5),
+)
 
 
 def tile_dividedspacetimeattention_pa_kernel(tc, x, Wq, bq, k, out):
@@ -42,7 +139,8 @@ def tile_dividedspacetimeattention_pa_kernel(tc, x, Wq, bq, k, out):
         ps_s = ctx.enter_context(tc.psum_pool(name="pss", bufs=2))
         ctx.enter_context(tc.manual_schedule())
 
-        wraw, kraw, wgs, wcs, kgs, kcs, qgs, qcs, ys, kts, scs = {}, {}, {}, {}, {}, {}, {}, {}, {}, {}, {}
+        wraw, kraw, wgs, wcs, kgs, kcs, qgs, qcs, ys, yfs, kts, scs = {}, {}, {}, {}, {}, {}, {}, {}, {}, {}, {}, {}
+        zts, ets, mxss, recs = {}, {}, {}, {}
 
         def copy_on(eng, dst, src):
             if eng == "v":
@@ -157,7 +255,8 @@ def tile_dividedspacetimeattention_pa_kernel(tc, x, Wq, bq, k, out):
                 quant(xg, xc, xs, c * 3072 + b * 1536, 1024)
                 quant(xg, xc, xs, c * 3072 + b * 1536 + 1024, 512)
 
-        def regroup(h, engines):
+        def regroup(h):
+            engines = REGROUP_ENGINES.get(h, REGROUP_DEFAULT)
             wg = wg_p.tile([P, 4096], BF16, align_bytes=64)
             dst = wg[:].rearrange("p (c e q i j) -> p c e q j i", c=2, e=2, q=64, i=4, j=4)
             src = wraw[h][:].rearrange("p (c j q i e) -> p c e q j i", c=2, j=4, q=64, i=4, e=2)
@@ -165,11 +264,15 @@ def tile_dividedspacetimeattention_pa_kernel(tc, x, Wq, bq, k, out):
                 copy_on(engines[n], dst[:, n // 2, n % 2], src[:, n // 2, n % 2])
             wgs[h] = wg
 
-        def quant_w(h):
+        def quant_w(h, pieces):
             wc = wq_p.tile([P, 1024], U32, align_bytes=64)
             ws = wq_p.tile([P, 1024], U8, align_bytes=64)
-            quant(wgs[h], wc, ws, 0, 4096)
+            for n in range(pieces):
+                quant(wgs[h], wc, ws, n * (4096 // pieces), 4096 // pieces)
             wcs[h] = (wc, ws)
+
+        def quant_w_whole(h):
+            quant_w(h, 1)
 
         def k_transposes(h):
             kw = kraw[h][:].bitcast(F32).rearrange("p (i w) -> p i w", i=6)
@@ -206,11 +309,18 @@ def tile_dividedspacetimeattention_pa_kernel(tc, x, Wq, bq, k, out):
                     mx(yv[:, j, :], wc, ws, c * 512 + tau * P, xc, xs, c * 768 + i * P, c == 0, c == 1)
             ys[(h, i)] = y
 
-        def ev(h, i, through_gpsimd):
+        def ev(h, i):
+            if h not in qgs:
+                qg = qg_p.tile([P, 3072], BF16, align_bytes=64)
+                qc = qq_p.tile([P, 768], U32, align_bytes=64)
+                qs = qq_p.tile([P, 768], U8, align_bytes=64)
+                qgs[h] = qg
+                qcs[h] = (qc, qs)
+            via = SG_FIRST if h == 0 else SG_LAST if h == LAST else SG_TILES
             y_rj = ys[(h, i)][:].rearrange("p (j r) -> p r j", j=4)
             q_rj = qgs[h][:, i * 512:(i + 1) * 512].rearrange("p (r j) -> p r j", j=4)
             b_rj = bias[:, h * 4:(h + 1) * 4].unsqueeze(1).to_broadcast([P, P, 4])
-            if through_gpsimd:
+            if i in via:
                 yf = yf_p.tile([P, 512], F32)
                 yf_rj = yf[:].rearrange("p (r j) -> p r j", j=4)
                 nc.scalar.copy(out=yf_rj, in_=y_rj)
@@ -218,17 +328,16 @@ def tile_dividedspacetimeattention_pa_kernel(tc, x, Wq, bq, k, out):
             else:
                 nc.vector.tensor_tensor(out=q_rj, in0=y_rj, in1=b_rj, op=ALU.add)
 
-        def new_q(h):
-            qg = qg_p.tile([P, 3072], BF16, align_bytes=64)
-            qc = qq_p.tile([P, 768], U32, align_bytes=64)
-            qs = qq_p.tile([P, 768], U8, align_bytes=64)
-            qgs[h] = qg
-            qcs[h] = (qc, qs)
-
         def quant_q(h, lo, width):
             quant(qgs[h], qcs[h][0], qcs[h][1], lo, width)
 
-        def s2(h, b):
+        def quant_q_a(h):
+            quant_q(h, 0, 2048)
+
+        def quant_q_b(h):
+            quant_q(h, 2048, 1024)
+
+        def s2b(h, b):
             qc, qs = qcs[h]
             kc, ks = kcs[h]
             sc = ps_s.tile([P, 384], F32, tag="s")
@@ -239,112 +348,81 @@ def tile_dividedspacetimeattention_pa_kernel(tc, x, Wq, bq, k, out):
                 mx(sc_v[:, s, :], mask_c, mask_s, 0, mask_c, mask_s, P, False, True)
             scs[(h, b)] = sc
 
-        def ex(h, b, dst):
+        def s2(h):
+            s2b(h, 0)
+            s2b(h, 1)
+
+        stage = {1: [], 2: [], 3: [], 4: [], 5: []}
+
+        def ex(h, b):
+            n = [m for m in range(len(BATCHES)) if BATCHES[m][0] <= h < BATCHES[m][1]][0]
+            h0, h1 = BATCHES[n]
+            if n not in zts:
+                zt = sm_p.tile([P, 384], F32)
+                zts[n] = zt
+            lo = b * (h1 - h0) * 48 + (h - h0) * 48
             nc.vector.tensor_reduce(
-                out=dst,
+                out=zts[n][:, lo:lo + 48].rearrange("p (t g) -> p t g", g=16),
                 in_=scs[(h, b)][:].rearrange("p (s a g) -> p s g a", s=3, a=8),
                 axis=AX.X,
                 op=ALU.max,
             )
+            if b == 1 and h == h1 - 1:
+                stage[1].append(n)
 
         out_v = out.rearrange("b h (s a) f g -> b (h s) (a f) g", s=3)
 
-        def softmax_a(z, e, groups, eng):
-            zg = z.rearrange("p (t g) -> p t g", g=16)
-            mxs = sm_p.tile([P, 24], F32)
-            nc.vector.tensor_reduce(out=mxs[:, 0:groups], in_=zg, axis=AX.X, op=ALU.max)
-            eng.tensor_tensor(out=zg, in0=zg, in1=mxs[:, 0:groups].unsqueeze(2).to_broadcast([P, groups, 16]), op=ALU.subtract)
-            nc.scalar.activation(out=e, in_=z, func=ACT.Exp, scale=SCALE)
-
-        def softmax_b(e, groups, eng):
-            eg = e.rearrange("p (t g) -> p t g", g=16)
-            sums = sm_p.tile([P, 24], F32)
-            nc.vector.tensor_reduce(out=sums[:, 0:groups], in_=eg, axis=AX.X, op=ALU.add)
-            rec = sm_p.tile([P, 24], F32)
-            nc.vector.reciprocal(out=rec[:, 0:groups], in_=sums[:, 0:groups])
-            eng.tensor_tensor(out=eg, in0=eg, in1=rec[:, 0:groups].unsqueeze(2).to_broadcast([P, groups, 16]), op=ALU.mult)
-
-        def store(e, b, h0, h1):
-            nc.sync.dma_start(out=out_v[b, h0 * 3:h1 * 3].rearrange("t p g -> p t g"), in_=e.rearrange("p (t g) -> p t g", g=16))
+        def softmax_stage(kk):
+            for n in stage[kk]:
+                h0, h1 = BATCHES[n]
+                groups = (h1 - h0) * 6
+                cols = groups * 16
+                eng = nc.vector if h1 == HEADS else nc.gpsimd
+                if kk == 1:
+                    mxs = sm_p.tile([P, 24], F32)
+                    mxss[n] = mxs
+                    nc.vector.tensor_reduce(out=mxs[:, 0:groups], in_=zts[n][:, 0:cols].rearrange("p (t g) -> p t g", g=16), axis=AX.X, op=ALU.max)
+                elif kk == 2:
+                    zg = zts[n][:, 0:cols].rearrange("p (t g) -> p t g", g=16)
+                    eng.tensor_tensor(out=zg, in0=zg, in1=mxss[n][:, 0:groups].unsqueeze(2).to_broadcast([P, groups, 16]), op=ALU.subtract)
+                elif kk == 3:
+                    et = sm_p.tile([P, 384], F32)
+                    ets[n] = et
+                    nc.scalar.activation(out=et[:, 0:cols], in_=zts[n][:, 0:cols], func=ACT.Exp, scale=SCALE)
+                elif kk == 4:
+                    eg = ets[n][:, 0:cols].rearrange("p (t g) -> p t g", g=16)
+                    sums = sm_p.tile([P, 24], F32)
+                    nc.vector.tensor_reduce(out=sums[:, 0:groups], in_=eg, axis=AX.X, op=ALU.add)
+                    rec = sm_p.tile([P, 24], F32)
+                    recs[n] = rec
+                    nc.vector.reciprocal(out=rec[:, 0:groups], in_=sums[:, 0:groups])
+                else:
+                    eg = ets[n][:, 0:cols].rearrange("p (t g) -> p t g", g=16)
+                    eng.tensor_tensor(out=eg, in0=eg, in1=recs[n][:, 0:groups].unsqueeze(2).to_broadcast([P, groups, 16]), op=ALU.mult)
+                    eb = ets[n][:, 0:cols].rearrange("p (b t g) -> p b t g", b=2, g=16)
+                    for b in range(2):
+                        nc.sync.dma_start(out=out_v[b, h0 * 3:h1 * 3].rearrange("t p g -> p t g"), in_=eb[:, b])
+                if kk < 5:
+                    stage[kk + 1].append(n)
+            stage[kk] = []
 
         prep_x(0)
-        regroup(0, ["v", "s", "v", "g"])
         quant_x(0)
-        quant_w(0)
+        regroup(0)
+        quant_w(0, 2)
         prep_x(1)
         quant_x(1)
-        regroup(1, ["s", "g", "s", "g"])
+        regroup(1)
 
-        zt, et, batch = None, None, None
+        emit = {
+            "lw": load_w, "lk": load_k, "mm": mm, "e": ev, "rg": regroup, "qw": quant_w_whole,
+            "kt": k_transposes, "ke": k_evac, "qk": quant_k, "qq": quant_q, "qqa": quant_q_a, "qqb": quant_q_b,
+            "s2": s2, "s2b": s2b, "ex": ex,
+        }
         for h in range(HEADS):
-            new_q(h)
-            if h + 4 < HEADS:
-                load_w(h + 4)
-            if h + 2 < HEADS:
-                load_k(h + 2)
-            for i in range(2):
-                mm(h, i)
-                ev(h, i, h > 0 and i in SG_TILES)
-            if h + 2 < HEADS:
-                regroup(h + 2, STEADY if h > 0 else ["s", "g", "s", "g"])
-            mm(h, 2)
-            ev(h, 2, h > 0 and 2 in SG_TILES)
-            finished = None
-            if h > 0:
-                for bt_ in BATCHES:
-                    if bt_[0] == h - 1:
-                        batch = bt_
-                        zt = sm_p.tile([P, 384], F32)
-                        et = sm_p.tile([P, 384], F32)
-                width = (batch[1] - batch[0]) * 48
-                s2(h - 1, 0)
-                s2(h - 1, 1)
-                for b in range(2):
-                    lo = b * width + (h - 1 - batch[0]) * 48
-                    ex(h - 1, b, zt[:, lo:lo + 48].rearrange("p (t g) -> p t g", g=16))
-                if batch[1] == h:
-                    finished = batch
-                    softmax_a(zt[:, 0:2 * width], et[:, 0:2 * width], width // 8, nc.gpsimd)
-            mm(h, 3)
-            ev(h, 3, False)
-            if h > 0:
-                k_transposes(h)
-                k_evac(h)
-            if h < LAST:
-                quant_w(h + 1)
-            else:
-                quant_q(h, 0, 1024)
-            mm(h, 4)
-            ev(h, 4, False)
-            if finished is not None:
-                width = (finished[1] - finished[0]) * 48
-                softmax_b(et[:, 0:2 * width], width // 8, nc.gpsimd)
-                for b in range(2):
-                    store(et[:, b * width:(b + 1) * width], b, finished[0], finished[1])
-            if h == LAST:
-                quant_q(h, 1024, 1024)
-                quant_k(h)
-            mm(h, 5)
-            ev(h, 5, False)
-            if h == 0:
-                k_transposes(0)
-                k_evac(0)
-            if h < LAST:
-                quant_q(h, 0, 2048)
-                quant_k(h)
-                quant_q(h, 2048, 1024)
-
-        zl = sm_p.tile([P, 96], F32)
-        el = sm_p.tile([P, 96], F32)
-        quant_q(LAST, 2048, 512)
-        s2(LAST, 0)
-        quant_q(LAST, 2560, 512)
-        ex(LAST, 0, zl[:, 0:48].rearrange("p (t g) -> p t g", g=16))
-        s2(LAST, 1)
-        softmax_a(zl[:, 0:48], el[:, 0:48], 3, nc.vector)
-        ex(LAST, 1, zl[:, 48:96].rearrange("p (t g) -> p t g", g=16))
-        softmax_a(zl[:, 48:96], el[:, 48:96], 3, nc.vector)
-        softmax_b(el[:, 0:48], 3, nc.vector)
-        store(el[:, 0:48], 0, LAST, HEADS)
-        softmax_b(el[:, 48:96], 3, nc.vector)
-        store(el[:, 48:96], 1, LAST, HEADS)
+            steps = FIRST_STEPS if h == 0 else LAST_STEPS if h == LAST else STEADY_STEPS
+            for step in steps:
+                if step[0] == "sm":
+                    softmax_stage(step[1])
+                elif 0 <= h + step[1] < HEADS:
+                    emit[step[0]](h + step[1], *step[2:])

@@ -25,91 +25,91 @@ SG_FIRST = ()
 SG_TILES = (0, 1)
 SG_LAST = (0, 1)
 STEADY_STEPS = (
-    ("lw", 4),
-    ("lk", 2),
-    ("mm", 0, 0),
-    ("e", 0, 0),
-    ("mm", 0, 1),
-    ("e", 0, 1),
-    ("sm", 4),
-    ("sm", 5),
-    ("rg", 2),
-    ("mm", 0, 2),
-    ("e", 0, 2),
-    ("s2", -1),
-    ("ex", -1, 0),
-    ("ex", -1, 1),
-    ("sm", 1),
-    ("sm", 2),
-    ("mm", 0, 3),
-    ("e", 0, 3),
-    ("kt", 0),
-    ("ke", 0),
-    ("sm", 3),
     ("qw", 1),
-    ("mm", 0, 4),
-    ("e", 0, 4),
+    ("mm", 0, 0),
+    ("mm", 0, 1),
+    ("e", 0, 0),
+    ("mm", 0, 2),
+    ("e", 0, 1),
     ("mm", 0, 5),
+    ("rg", 2),
+    ("e", 0, 2),
+    ("lw", 4),
+    ("sm", 4),
+    ("mm", 0, 4),
+    ("s2", -1),
+    ("mm", 0, 3),
+    ("ex", -1, 0),
+    ("sm", 1),
+    ("sm", 5),
+    ("e", 0, 4),
+    ("sm", 3),
+    ("kt", 0),
     ("e", 0, 5),
-    ("qqa", 0),
-    ("qk", 0),
+    ("lk", 2),
+    ("e", 0, 3),
+    ("ex", -1, 1),
     ("qqb", 0),
+    ("sm", 2),
+    ("qqa", 0),
+    ("ke", 0),
+    ("qk", 0),
 )
 FIRST_STEPS = (
-    ("lw", 4),
-    ("lk", 2),
     ("mm", 0, 0),
     ("e", 0, 0),
+    ("mm", 0, 2),
     ("mm", 0, 1),
     ("e", 0, 1),
-    ("rg", 2),
-    ("mm", 0, 2),
-    ("e", 0, 2),
     ("mm", 0, 3),
+    ("e", 0, 2),
+    ("lk", 2),
+    ("mm", 0, 5),
     ("e", 0, 3),
     ("qw", 1),
     ("mm", 0, 4),
-    ("e", 0, 4),
-    ("mm", 0, 5),
     ("e", 0, 5),
+    ("rg", 2),
     ("kt", 0),
+    ("e", 0, 4),
     ("ke", 0),
-    ("qqa", 0),
     ("qqb", 0),
+    ("qqa", 0),
     ("qk", 0),
+    ("lw", 4),
 )
 LAST_STEPS = (
-    ("mm", 0, 0),
-    ("e", 0, 0),
-    ("mm", 0, 1),
-    ("e", 0, 1),
     ("sm", 4),
-    ("sm", 5),
+    ("mm", 0, 1),
+    ("mm", 0, 0),
     ("mm", 0, 2),
     ("e", 0, 2),
+    ("e", 0, 0),
     ("s2", -1),
-    ("ex", -1, 0),
     ("ex", -1, 1),
+    ("ex", -1, 0),
     ("sm", 1),
-    ("sm", 2),
+    ("e", 0, 1),
+    ("mm", 0, 5),
+    ("sm", 5),
+    ("e", 0, 5),
     ("mm", 0, 3),
     ("e", 0, 3),
-    ("kt", 0),
-    ("ke", 0),
-    ("sm", 3),
-    ("qq", 0, 0, 1024),
+    ("sm", 2),
     ("mm", 0, 4),
+    ("kt", 0),
     ("e", 0, 4),
-    ("qq", 0, 1024, 1024),
-    ("sm", 4),
-    ("sm", 5),
-    ("mm", 0, 5),
-    ("e", 0, 5),
-    ("qk", 0),
-    ("qq", 0, 2048, 512),
-    ("s2b", 0, 0),
+    ("ke", 0),
+    ("qq", 0, 0, 1024),
     ("qq", 0, 2560, 512),
+    ("qq", 0, 1024, 1024),
+    ("qk", 0),
+    ("s2b", 0, 0),
+    ("sm", 3),
+    ("qq", 0, 2048, 512),
+    ("sm", 4),
     ("ex", 0, 0),
+    ("sm", 5),
     ("s2b", 0, 1),
     ("ex", 0, 1),
     ("sm", 1),
@@ -353,6 +353,7 @@ def tile_dividedspacetimeattention_pa_kernel(tc, x, Wq, bq, k, out):
             s2b(h, 1)
 
         stage = {1: [], 2: [], 3: [], 4: [], 5: []}
+        extracted = set()
 
         def ex(h, b):
             n = [m for m in range(len(BATCHES)) if BATCHES[m][0] <= h < BATCHES[m][1]][0]
@@ -367,7 +368,8 @@ def tile_dividedspacetimeattention_pa_kernel(tc, x, Wq, bq, k, out):
                 axis=AX.X,
                 op=ALU.max,
             )
-            if b == 1 and h == h1 - 1:
+            extracted.add((h, b))
+            if h == h1 - 1 and (h, 1 - b) in extracted:
                 stage[1].append(n)
 
         out_v = out.rearrange("b h (s a) f g -> b (h s) (a f) g", s=3)

@@ -15,201 +15,100 @@ AX = mybir.AxisListType
 P = 128
 HEADS = 12
 LAST = HEADS - 1
+TILES = 6
 FLOPS = 2 * 768 * 1024 * 6144 + 2 * 576 * 16 * 16 * 512
 SCALE = 1.0 / 96.0
-BIG = 2.0 ** 100
+OFF_BLOCK = 2.0 ** 100
+VIA_GPSIMD = (0, 1)
 BATCHES = ((0, 4), (4, 8), (8, 11), (11, 12))
-REGROUP_ENGINES = {0: "vsvs", 1: "sssg", 2: "sgsg"}
-REGROUP_DEFAULT = "sssg"
-SG_FIRST = ()
-SG_TILES = (0, 1)
-SG_LAST = (0, 1)
-STEADY_STEPS = (
-    ("qw", 1),
-    ("mm", 0, 0),
-    ("mm", 0, 1),
-    ("e", 0, 0),
-    ("mm", 0, 2),
-    ("e", 0, 1),
-    ("mm", 0, 5),
-    ("rg", 2),
-    ("e", 0, 2),
-    ("lw", 4),
-    ("sm", 4),
-    ("mm", 0, 4),
-    ("s2", -1),
-    ("mm", 0, 3),
-    ("ex", -1, 0),
-    ("sm", 1),
-    ("sm", 5),
-    ("e", 0, 4),
-    ("sm", 3),
-    ("kt", 0),
-    ("e", 0, 5),
-    ("lk", 2),
-    ("e", 0, 3),
-    ("ex", -1, 1),
-    ("qqb", 0),
-    ("sm", 2),
-    ("qqa", 0),
-    ("ke", 0),
-    ("qk", 0),
-)
-FIRST_STEPS = (
-    ("mm", 0, 0),
-    ("e", 0, 0),
-    ("mm", 0, 2),
-    ("mm", 0, 1),
-    ("e", 0, 1),
-    ("mm", 0, 3),
-    ("e", 0, 2),
-    ("lk", 2),
-    ("mm", 0, 5),
-    ("e", 0, 3),
-    ("qw", 1),
-    ("mm", 0, 4),
-    ("e", 0, 5),
-    ("rg", 2),
-    ("kt", 0),
-    ("e", 0, 4),
-    ("ke", 0),
-    ("qqb", 0),
-    ("qqa", 0),
-    ("qk", 0),
-    ("lw", 4),
-)
-LAST_STEPS = (
-    ("sm", 4),
-    ("mm", 0, 1),
-    ("mm", 0, 0),
-    ("mm", 0, 2),
-    ("e", 0, 2),
-    ("e", 0, 0),
-    ("s2", -1),
-    ("ex", -1, 1),
-    ("ex", -1, 0),
-    ("sm", 1),
-    ("e", 0, 1),
-    ("mm", 0, 5),
-    ("sm", 5),
-    ("e", 0, 5),
-    ("mm", 0, 3),
-    ("e", 0, 3),
-    ("sm", 2),
-    ("mm", 0, 4),
-    ("kt", 0),
-    ("e", 0, 4),
-    ("ke", 0),
-    ("qq", 0, 0, 1024),
-    ("qq", 0, 2560, 512),
-    ("qq", 0, 1024, 1024),
-    ("qk", 0),
-    ("s2b", 0, 0),
-    ("sm", 3),
-    ("qq", 0, 2048, 512),
-    ("sm", 4),
-    ("ex", 0, 0),
-    ("sm", 5),
-    ("s2b", 0, 1),
-    ("ex", 0, 1),
-    ("sm", 1),
-    ("sm", 2),
-    ("sm", 3),
-    ("sm", 4),
-    ("sm", 5),
-)
 
 
 def tile_dividedspacetimeattention_pa_kernel(tc, x, Wq, bq, k, out):
     nc = tc.nc
     with ExitStack() as ctx:
         consts = ctx.enter_context(tc.tile_pool(name="consts", bufs=1))
-        wraw_p = ctx.enter_context(tc.tile_pool(name="wraw", bufs=4))
-        kraw_p = ctx.enter_context(tc.tile_pool(name="kraw", bufs=3))
-        wg_p = ctx.enter_context(tc.tile_pool(name="wg", bufs=3))
-        wq_p = ctx.enter_context(tc.tile_pool(name="wq", bufs=2))
-        kg_p = ctx.enter_context(tc.tile_pool(name="kg", bufs=2))
-        kq_p = ctx.enter_context(tc.tile_pool(name="kq", bufs=2))
-        qg_p = ctx.enter_context(tc.tile_pool(name="qg", bufs=2))
-        qq_p = ctx.enter_context(tc.tile_pool(name="qq", bufs=2))
-        yf_p = ctx.enter_context(tc.tile_pool(name="yf", bufs=2))
-        sm_p = ctx.enter_context(tc.tile_pool(name="sm", bufs=2))
-        ps_y = ctx.enter_context(tc.psum_pool(name="psy", bufs=3))
-        ps_t = ctx.enter_context(tc.psum_pool(name="pst", bufs=3))
-        ps_s = ctx.enter_context(tc.psum_pool(name="pss", bufs=2))
+        w_raw_pool = ctx.enter_context(tc.tile_pool(name="w_raw", bufs=4))
+        k_raw_pool = ctx.enter_context(tc.tile_pool(name="k_raw", bufs=3))
+        w_grouped_pool = ctx.enter_context(tc.tile_pool(name="w_grouped", bufs=2))
+        w_mx_pool = ctx.enter_context(tc.tile_pool(name="w_mx", bufs=2))
+        k_grouped_pool = ctx.enter_context(tc.tile_pool(name="k_grouped", bufs=2))
+        k_mx_pool = ctx.enter_context(tc.tile_pool(name="k_mx", bufs=2))
+        q_grouped_pool = ctx.enter_context(tc.tile_pool(name="q_grouped", bufs=2))
+        q_mx_pool = ctx.enter_context(tc.tile_pool(name="q_mx", bufs=2))
+        y_copy_pool = ctx.enter_context(tc.tile_pool(name="y_copy", bufs=2))
+        soft_pool = ctx.enter_context(tc.tile_pool(name="soft", bufs=2))
+        y_psum = ctx.enter_context(tc.psum_pool(name="y_psum", bufs=3))
+        t_psum = ctx.enter_context(tc.psum_pool(name="t_psum", bufs=3))
+        s_psum = ctx.enter_context(tc.psum_pool(name="s_psum", bufs=2))
         ctx.enter_context(tc.manual_schedule())
 
-        wraw, kraw, wgs, wcs, kgs, kcs, qgs, qcs, ys, yfs, kts, scs = {}, {}, {}, {}, {}, {}, {}, {}, {}, {}, {}, {}
-        zts, ets, mxss, recs = {}, {}, {}, {}
+        w_raw, k_raw, w_grouped, w_mx, k_banks, k_grouped, k_mx = {}, {}, {}, {}, {}, {}, {}
+        q_grouped, q_mx, y_banks, score_banks = {}, {}, {}, {}
+        scores, exps, maxima, reciprocals = {}, {}, {}, {}
 
-        def copy_on(eng, dst, src):
-            if eng == "v":
-                nc.vector.tensor_copy(out=dst, in_=src)
-            elif eng == "s":
-                nc.scalar.copy(out=dst, in_=src)
-            else:
-                nc.gpsimd.tensor_scalar(out=dst, in0=src, scalar1=1.0, scalar2=0.0, op0=ALU.mult, op1=ALU.add)
-
-        def quant(src, codes, scales, lo, width):
+        def quantise(src, mx_pair, first, width):
+            words, scale_bytes = mx_pair
             nc.vector.quantize_mx(
-                out=codes[:, lo // 4:(lo + width) // 4].bitcast(FP8X4),
-                scales=scales[:, lo // 4:(lo + width) // 4],
-                in_=src[:, lo:lo + width],
+                out=words[:, first // 4:(first + width) // 4].bitcast(FP8X4),
+                scales=scale_bytes[:, first // 4:(first + width) // 4],
+                in_=src[:, first:first + width],
             )
 
-        def mx(dst, a, a_s, a0, b, b_s, b0, start, stop):
+        def mx_pass(dst, stationary, m0, moving, n0, start, stop):
             nc.tensor.matmul_mx(
                 out=dst,
-                lhsT=a[:, a0:a0 + P].bitcast(FP8X4),
-                lhsT_scale=a_s[:, a0:a0 + P],
-                rhs=b[:, b0:b0 + P].bitcast(FP8X4),
-                rhs_scale=b_s[:, b0:b0 + P],
+                lhsT=stationary[0][:, m0:m0 + P].bitcast(FP8X4),
+                lhsT_scale=stationary[1][:, m0:m0 + P],
+                rhs=moving[0][:, n0:n0 + P].bitcast(FP8X4),
+                rhs_scale=moving[1][:, n0:n0 + P],
                 start=start,
                 stop=stop,
             )
 
         def load_w(h):
-            w_raw = wraw_p.tile([P, 4096], BF16)
-            wv = w_raw[:].rearrange("p (c j w) -> p c j w", c=2, j=4)
+            raw = w_raw_pool.tile([P, 4096], BF16)
+            rows = raw[:].rearrange("p (c j w) -> p c j w", c=2, j=4)
             for c in range(2):
                 for u in range(2):
                     r0 = 512 * c + 256 * u
                     nc.sync.dma_start(
-                        out=wv[:, c, 2 * u:2 * u + 2, :],
+                        out=rows[:, c, 2 * u:2 * u + 2, :],
                         in_=Wq[r0:r0 + 256, h * 512:(h + 1) * 512].rearrange("(p e) w -> p e w", e=2),
                     )
-            wraw[h] = w_raw
+            w_raw[h] = raw
 
         k_rows = k.rearrange("b h n g d -> b h (n g) d")
 
         def load_k(h):
-            k_raw = kraw_p.tile([P, 3072], BF16)
-            kv = k_raw[:].rearrange("p (i d) -> p i d", i=6)
+            raw = k_raw_pool.tile([P, 3072], BF16)
+            tiles = raw[:].rearrange("p (i d) -> p i d", i=TILES)
             for b in range(2):
                 nc.sync.dma_start(
-                    out=kv[:, 3 * b:3 * b + 3, :],
+                    out=tiles[:, 3 * b:3 * b + 3, :],
                     in_=k_rows[b, h].rearrange("(s p) d -> p s d", s=3),
                 )
-            kraw[h] = k_raw
-
-        ident = consts.tile([P, P], F32)
-        make_identity(nc, ident[:])
-        warm = consts.tile([P, 2], F32)
-        nc.vector.memset(warm[:], 0.0)
-        nc.scalar.activation(out=warm[:, 1:2], in_=warm[:, 0:1], func=ACT.Exp)
-        b_raw = consts.tile([P, 256], BF16)
-        nc.vector.memset(b_raw[:], 0.0)
-        mask_in = consts.tile([P, 1024], BF16, align_bytes=64)
-        nc.vector.memset(mask_in[:], 0.0)
+            k_raw[h] = raw
 
         x_raw = consts.tile([P, 6144], BF16)
-        xr_v = x_raw[:].rearrange("p (b r c) -> p b r c", b=2, r=3)
 
         def load_x(b):
-            nc.sync.dma_start(out=xr_v[:, b], in_=x[b].rearrange("(p r) c -> p r c", r=3))
+            nc.sync.dma_start(
+                out=x_raw[:].rearrange("p (b r c) -> p b r c", b=2, r=3)[:, b],
+                in_=x[b].rearrange("(p r) c -> p r c", r=3),
+            )
+
+        identity = consts.tile([P, P], F32)
+        make_identity(nc, identity[:])
+        table_warmer = consts.tile([P, 2], F32)
+        nc.vector.memset(table_warmer[:], 0.0)
+        nc.scalar.activation(out=table_warmer[:, 1:2], in_=table_warmer[:, 0:1], func=ACT.Exp)
+        bias_rows = consts.tile([P, 256], BF16)
+        nc.vector.memset(bias_rows[:], 0.0)
+        mask_values = consts.tile([P, 1024], BF16, align_bytes=64)
+        nc.vector.memset(mask_values[:], 0.0)
 
         load_x(0)
-        nc.sync.dma_start(out=b_raw[0:24, :], in_=bq.rearrange("(r c) -> r c", c=256))
+        nc.sync.dma_start(out=bias_rows[0:24, :], in_=bq.rearrange("(r c) -> r c", c=256))
         load_w(0)
         load_x(1)
         load_w(1)
@@ -218,213 +117,258 @@ def tile_dividedspacetimeattention_pa_kernel(tc, x, Wq, bq, k, out):
         load_w(3)
         load_k(1)
 
-        mv = mask_in[:].rearrange("p (o a f j) -> p o a f j", o=2, a=8, f=16)
-        eye8 = ident[:, 0:8].unsqueeze(2).to_broadcast([P, 8, 16])
-        nc.vector.tensor_copy(out=mv[:, 0, :, :, 0], in_=eye8)
-        nc.vector.tensor_scalar(out=mv[:, 1, :, :, 0], in0=eye8, scalar1=-1.0, scalar2=BIG, op0=ALU.add, op1=ALU.mult)
-        mask_c = consts.tile([P, 256], U32, align_bytes=64)
-        mask_s = consts.tile([P, 256], U8, align_bytes=64)
-        quant(mask_in, mask_c, mask_s, 0, 1024)
+        mask_slots = mask_values[:].rearrange("p (o a f j) -> p o a f j", o=2, a=8, f=16)
+        same_patch = identity[:, 0:8].unsqueeze(2).to_broadcast([P, 8, 16])
+        nc.vector.tensor_copy(out=mask_slots[:, 0, :, :, 0], in_=same_patch)
+        nc.vector.tensor_scalar(
+            out=mask_slots[:, 1, :, :, 0], in0=same_patch, scalar1=-1.0, scalar2=OFF_BLOCK, op0=ALU.add, op1=ALU.mult
+        )
+        mask_words = consts.tile([P, 256], U32, align_bytes=64)
+        mask_scales = consts.tile([P, 256], U8, align_bytes=64)
+        mask_mx = (mask_words, mask_scales)
+        quantise(mask_values, mask_mx, 0, 1024)
 
-        bt = ps_t.tile([P, 512], F32, tag="t")
-        nc.tensor.transpose(bt[:, 0:P], b_raw[:].bitcast(F32), ident[:])
+        bias_bank = t_psum.tile([P, 512], F32, tag="t")
+        nc.tensor.transpose(bias_bank[:, 0:P], bias_rows[:].bitcast(F32), identity[:])
         bias = consts.tile([P, 48], F32)
-        nc.vector.tensor_copy(out=bias[:], in_=bt[:, 0:24].bitcast(BF16))
+        nc.vector.tensor_copy(out=bias[:], in_=bias_bank[:, 0:24].bitcast(BF16))
 
-        xw = x_raw[:].bitcast(F32).rearrange("p (b r w) -> p b r w", b=2, r=3)
-        xg = consts.tile([P, 6144], BF16, align_bytes=64)
-        xg_w = xg[:].bitcast(F32).rearrange("p (c n f u) -> p c n f u", c=2, n=48, f=16)
-        xc = consts.tile([P, 1536], U32, align_bytes=64)
-        xs = consts.tile([P, 1536], U8, align_bytes=64)
+        x_words = x_raw[:].bitcast(F32).rearrange("p (b r w) -> p b r w", b=2, r=3)
+        x_grouped = consts.tile([P, 6144], BF16, align_bytes=64)
+        x_grouped_words = x_grouped[:].bitcast(F32).rearrange("p (c n f u) -> p c n f u", c=2, n=48, f=16)
+        x_codes = consts.tile([P, 1536], U32, align_bytes=64)
+        x_scales = consts.tile([P, 1536], U8, align_bytes=64)
+        x_mx = (x_codes, x_scales)
 
-        def prep_x(b):
+        def transpose_x(b):
             for r in range(3):
-                xt = ps_t.tile([P, 512], F32, tag="t")
-                xt_v = xt[:].rearrange("p (q t) -> p q t", q=4)
+                bank = t_psum.tile([P, 512], F32, tag="t")
+                halves = bank[:].rearrange("p (q t) -> p q t", q=4)
                 for q in range(4):
-                    nc.tensor.transpose(xt_v[:, q, :], xw[:, b, r, q * P:(q + 1) * P], ident[:])
+                    nc.tensor.transpose(halves[:, q, :], x_words[:, b, r, q * P:(q + 1) * P], identity[:])
                 for c in range(2):
-                    copy_on(
-                        "v" if c == 0 else "s",
-                        xg_w[:, c, b * 24 + r:(b + 1) * 24:3, :, :],
-                        xt_v[:, 2 * c:2 * c + 2, :].rearrange("p u (f a) -> p a f u", a=8),
-                    )
+                    dst = x_grouped_words[:, c, b * 24 + r:(b + 1) * 24:3, :, :]
+                    src = halves[:, 2 * c:2 * c + 2, :].rearrange("p u (f a) -> p a f u", a=8)
+                    if c == 0:
+                        nc.vector.tensor_copy(out=dst, in_=src)
+                    else:
+                        nc.scalar.copy(out=dst, in_=src)
 
-        def quant_x(b):
+        def quantise_x(b):
             for c in range(2):
-                quant(xg, xc, xs, c * 3072 + b * 1536, 1024)
-                quant(xg, xc, xs, c * 3072 + b * 1536 + 1024, 512)
+                quantise(x_grouped, x_mx, c * 3072 + b * 1536, 1024)
+                quantise(x_grouped, x_mx, c * 3072 + b * 1536 + 1024, 512)
 
-        def regroup(h):
-            engines = REGROUP_ENGINES.get(h, REGROUP_DEFAULT)
-            wg = wg_p.tile([P, 4096], BF16, align_bytes=64)
-            dst = wg[:].rearrange("p (c e q i j) -> p c e q j i", c=2, e=2, q=64, i=4, j=4)
-            src = wraw[h][:].rearrange("p (c j q i e) -> p c e q j i", c=2, j=4, q=64, i=4, e=2)
-            for n in range(4):
-                copy_on(engines[n], dst[:, n // 2, n % 2], src[:, n // 2, n % 2])
-            wgs[h] = wg
+        def regroup_w(h):
+            grouped = w_grouped_pool.tile([P, 4096], BF16, align_bytes=64)
+            dst = grouped[:].rearrange("p (c e v i j) -> p c e v j i", c=2, e=2, v=64, i=4, j=4)
+            src = w_raw[h][:].rearrange("p (c j v i e) -> p c e v j i", c=2, j=4, v=64, i=4, e=2)
+            for c in range(2):
+                for e in range(2):
+                    if h == 0 and e == 0:
+                        nc.vector.tensor_copy(out=dst[:, c, e], in_=src[:, c, e])
+                    elif h > 0 and c == 1 and e == 1:
+                        nc.gpsimd.tensor_scalar(
+                            out=dst[:, c, e], in0=src[:, c, e], scalar1=1.0, scalar2=0.0, op0=ALU.mult, op1=ALU.add
+                        )
+                    else:
+                        nc.scalar.copy(out=dst[:, c, e], in_=src[:, c, e])
+            w_grouped[h] = grouped
 
-        def quant_w(h, pieces):
-            wc = wq_p.tile([P, 1024], U32, align_bytes=64)
-            ws = wq_p.tile([P, 1024], U8, align_bytes=64)
-            for n in range(pieces):
-                quant(wgs[h], wc, ws, n * (4096 // pieces), 4096 // pieces)
-            wcs[h] = (wc, ws)
+        def quantise_w(h, calls):
+            words = w_mx_pool.tile([P, 1024], U32, align_bytes=64)
+            scale_bytes = w_mx_pool.tile([P, 1024], U8, align_bytes=64)
+            w_mx[h] = (words, scale_bytes)
+            for n in range(calls):
+                quantise(w_grouped[h], w_mx[h], n * (4096 // calls), 4096 // calls)
 
-        def quant_w_whole(h):
-            quant_w(h, 1)
-
-        def k_transposes(h):
-            kw = kraw[h][:].bitcast(F32).rearrange("p (i w) -> p i w", i=6)
-            kts[h] = []
-            for jj in range(3):
-                kt = ps_t.tile([P, 512], F32, tag="t")
-                kt_v = kt[:].rearrange("p (i u r) -> p i u r", i=2, u=2)
-                for ii in range(2):
+        def transpose_k(h):
+            words = k_raw[h][:].bitcast(F32).rearrange("p (i w) -> p i w", i=TILES)
+            k_banks[h] = []
+            for pair in range(3):
+                bank = t_psum.tile([P, 512], F32, tag="t")
+                halves = bank[:].rearrange("p (i u r) -> p i u r", i=2, u=2)
+                for i in range(2):
                     for u in range(2):
-                        nc.tensor.transpose(kt_v[:, ii, u, :], kw[:, 2 * jj + ii, u * P:(u + 1) * P], ident[:])
-                kts[h].append(kt_v)
+                        nc.tensor.transpose(halves[:, i, u, :], words[:, 2 * pair + i, u * P:(u + 1) * P], identity[:])
+                k_banks[h].append(halves)
 
-        def k_evac(h):
-            kg = kg_p.tile([P, 3072], BF16, align_bytes=64)
-            kg_w = kg[:].bitcast(F32).rearrange("p (i r u) -> p i r u", i=6, u=2)
-            for jj in range(3):
-                nc.scalar.copy(out=kg_w[:, 2 * jj:2 * jj + 2], in_=kts[h][jj].rearrange("p i u r -> p i r u"))
-            kgs[h] = kg
+        def regroup_k(h):
+            grouped = k_grouped_pool.tile([P, 3072], BF16, align_bytes=64)
+            grouped_words = grouped[:].bitcast(F32).rearrange("p (i r u) -> p i r u", i=TILES, u=2)
+            for pair in range(3):
+                nc.scalar.copy(
+                    out=grouped_words[:, 2 * pair:2 * pair + 2], in_=k_banks[h][pair].rearrange("p i u r -> p i r u")
+                )
+            k_grouped[h] = grouped
 
-        def quant_k(h):
-            kc = kq_p.tile([P, 768], U32, align_bytes=64)
-            ks = kq_p.tile([P, 768], U8, align_bytes=64)
-            quant(kgs[h], kc, ks, 0, 2048)
-            quant(kgs[h], kc, ks, 2048, 1024)
-            kcs[h] = (kc, ks)
+        def quantise_k(h):
+            words = k_mx_pool.tile([P, 768], U32, align_bytes=64)
+            scale_bytes = k_mx_pool.tile([P, 768], U8, align_bytes=64)
+            k_mx[h] = (words, scale_bytes)
+            quantise(k_grouped[h], k_mx[h], 0, 2048)
+            quantise(k_grouped[h], k_mx[h], 2048, 1024)
 
-        def mm(h, i):
-            wc, ws = wcs[h]
-            y = ps_y.tile([P, 512], F32, tag="y")
-            yv = y[:].rearrange("p (j r) -> p j r", j=4)
+        def project(h, i):
+            bank = y_psum.tile([P, 512], F32, tag="y")
+            slots = bank[:].rearrange("p (j r) -> p j r", j=4)
             for j in range(4):
-                tau = 2 * (j % 2) + j // 2
+                output_tile = 2 * (j % 2) + j // 2
                 for c in range(2):
-                    mx(yv[:, j, :], wc, ws, c * 512 + tau * P, xc, xs, c * 768 + i * P, c == 0, c == 1)
-            ys[(h, i)] = y
+                    mx_pass(slots[:, j, :], w_mx[h], c * 512 + output_tile * P, x_mx, c * 768 + i * P, c == 0, c == 1)
+            y_banks[(h, i)] = bank
 
-        def ev(h, i):
-            if h not in qgs:
-                qg = qg_p.tile([P, 3072], BF16, align_bytes=64)
-                qc = qq_p.tile([P, 768], U32, align_bytes=64)
-                qs = qq_p.tile([P, 768], U8, align_bytes=64)
-                qgs[h] = qg
-                qcs[h] = (qc, qs)
-            via = SG_FIRST if h == 0 else SG_LAST if h == LAST else SG_TILES
-            y_rj = ys[(h, i)][:].rearrange("p (j r) -> p r j", j=4)
-            q_rj = qgs[h][:, i * 512:(i + 1) * 512].rearrange("p (r j) -> p r j", j=4)
-            b_rj = bias[:, h * 4:(h + 1) * 4].unsqueeze(1).to_broadcast([P, P, 4])
-            if i in via:
-                yf = yf_p.tile([P, 512], F32)
-                yf_rj = yf[:].rearrange("p (r j) -> p r j", j=4)
-                nc.scalar.copy(out=yf_rj, in_=y_rj)
-                nc.gpsimd.tensor_tensor(out=q_rj, in0=yf_rj, in1=b_rj, op=ALU.add)
+        def new_q(h):
+            grouped = q_grouped_pool.tile([P, 3072], BF16, align_bytes=64)
+            words = q_mx_pool.tile([P, 768], U32, align_bytes=64)
+            scale_bytes = q_mx_pool.tile([P, 768], U8, align_bytes=64)
+            q_grouped[h] = grouped
+            q_mx[h] = (words, scale_bytes)
+
+        def round_q(h, i):
+            y_by_token = y_banks[(h, i)][:].rearrange("p (j r) -> p r j", j=4)
+            q_by_token = q_grouped[h][:, i * 512:(i + 1) * 512].rearrange("p (r j) -> p r j", j=4)
+            bias_by_token = bias[:, h * 4:(h + 1) * 4].unsqueeze(1).to_broadcast([P, P, 4])
+            if h > 0 and i in VIA_GPSIMD:
+                y_copy = y_copy_pool.tile([P, 512], F32)
+                y_copy_by_token = y_copy[:].rearrange("p (r j) -> p r j", j=4)
+                nc.scalar.copy(out=y_copy_by_token, in_=y_by_token)
+                nc.gpsimd.tensor_tensor(out=q_by_token, in0=y_copy_by_token, in1=bias_by_token, op=ALU.add)
             else:
-                nc.vector.tensor_tensor(out=q_rj, in0=y_rj, in1=b_rj, op=ALU.add)
+                nc.vector.tensor_tensor(out=q_by_token, in0=y_by_token, in1=bias_by_token, op=ALU.add)
 
-        def quant_q(h, lo, width):
-            quant(qgs[h], qcs[h][0], qcs[h][1], lo, width)
+        def multiply_qk(h):
+            for b in range(2):
+                bank = s_psum.tile([P, 384], F32, tag="s")
+                tiles = bank[:].rearrange("p (s c) -> p s c", s=3)
+                for s in range(3):
+                    i = 3 * b + s
+                    mx_pass(tiles[:, s, :], q_mx[h], i * P, k_mx[h], i * P, True, False)
+                    mx_pass(tiles[:, s, :], mask_mx, 0, mask_mx, P, False, True)
+                score_banks[(h, b)] = bank
 
-        def quant_q_a(h):
-            quant_q(h, 0, 2048)
+        def batch_of(h):
+            return [n for n in range(len(BATCHES)) if BATCHES[n][0] <= h < BATCHES[n][1]][0]
 
-        def quant_q_b(h):
-            quant_q(h, 2048, 1024)
-
-        def s2b(h, b):
-            qc, qs = qcs[h]
-            kc, ks = kcs[h]
-            sc = ps_s.tile([P, 384], F32, tag="s")
-            sc_v = sc[:].rearrange("p (s c) -> p s c", s=3)
-            for s in range(3):
-                i = 3 * b + s
-                mx(sc_v[:, s, :], qc, qs, i * P, kc, ks, i * P, True, False)
-                mx(sc_v[:, s, :], mask_c, mask_s, 0, mask_c, mask_s, P, False, True)
-            scs[(h, b)] = sc
-
-        def s2(h):
-            s2b(h, 0)
-            s2b(h, 1)
-
-        stage = {1: [], 2: [], 3: [], 4: [], 5: []}
-        extracted = set()
-
-        def ex(h, b):
-            n = [m for m in range(len(BATCHES)) if BATCHES[m][0] <= h < BATCHES[m][1]][0]
+        def extract(h, b):
+            n = batch_of(h)
             h0, h1 = BATCHES[n]
-            if n not in zts:
-                zt = sm_p.tile([P, 384], F32)
-                zts[n] = zt
-            lo = b * (h1 - h0) * 48 + (h - h0) * 48
+            if n not in scores:
+                batch_scores = soft_pool.tile([P, 384], F32)
+                scores[n] = batch_scores
+            first = (b * (h1 - h0) + h - h0) * 48
             nc.vector.tensor_reduce(
-                out=zts[n][:, lo:lo + 48].rearrange("p (t g) -> p t g", g=16),
-                in_=scs[(h, b)][:].rearrange("p (s a g) -> p s g a", s=3, a=8),
+                out=scores[n][:, first:first + 48].rearrange("p (s g) -> p s g", g=16),
+                in_=score_banks[(h, b)][:].rearrange("p (s a g) -> p s g a", s=3, a=8),
                 axis=AX.X,
                 op=ALU.max,
             )
-            extracted.add((h, b))
-            if h == h1 - 1 and (h, 1 - b) in extracted:
-                stage[1].append(n)
 
-        out_v = out.rearrange("b h (s a) f g -> b (h s) (a f) g", s=3)
+        def rows_of(n):
+            return (BATCHES[n][1] - BATCHES[n][0]) * TILES
 
-        def softmax_stage(kk):
-            for n in stage[kk]:
-                h0, h1 = BATCHES[n]
-                groups = (h1 - h0) * 6
-                cols = groups * 16
-                eng = nc.vector if h1 == HEADS else nc.gpsimd
-                if kk == 1:
-                    mxs = sm_p.tile([P, 24], F32)
-                    mxss[n] = mxs
-                    nc.vector.tensor_reduce(out=mxs[:, 0:groups], in_=zts[n][:, 0:cols].rearrange("p (t g) -> p t g", g=16), axis=AX.X, op=ALU.max)
-                elif kk == 2:
-                    zg = zts[n][:, 0:cols].rearrange("p (t g) -> p t g", g=16)
-                    eng.tensor_tensor(out=zg, in0=zg, in1=mxss[n][:, 0:groups].unsqueeze(2).to_broadcast([P, groups, 16]), op=ALU.subtract)
-                elif kk == 3:
-                    et = sm_p.tile([P, 384], F32)
-                    ets[n] = et
-                    nc.scalar.activation(out=et[:, 0:cols], in_=zts[n][:, 0:cols], func=ACT.Exp, scale=SCALE)
-                elif kk == 4:
-                    eg = ets[n][:, 0:cols].rearrange("p (t g) -> p t g", g=16)
-                    sums = sm_p.tile([P, 24], F32)
-                    nc.vector.tensor_reduce(out=sums[:, 0:groups], in_=eg, axis=AX.X, op=ALU.add)
-                    rec = sm_p.tile([P, 24], F32)
-                    recs[n] = rec
-                    nc.vector.reciprocal(out=rec[:, 0:groups], in_=sums[:, 0:groups])
-                else:
-                    eg = ets[n][:, 0:cols].rearrange("p (t g) -> p t g", g=16)
-                    eng.tensor_tensor(out=eg, in0=eg, in1=recs[n][:, 0:groups].unsqueeze(2).to_broadcast([P, groups, 16]), op=ALU.mult)
-                    eb = ets[n][:, 0:cols].rearrange("p (b t g) -> p b t g", b=2, g=16)
-                    for b in range(2):
-                        nc.sync.dma_start(out=out_v[b, h0 * 3:h1 * 3].rearrange("t p g -> p t g"), in_=eb[:, b])
-                if kk < 5:
-                    stage[kk + 1].append(n)
-            stage[kk] = []
+        def by_row(tile_of_batch, n):
+            return tile_of_batch[:, 0:rows_of(n) * 16].rearrange("p (t g) -> p t g", g=16)
 
-        prep_x(0)
-        quant_x(0)
-        regroup(0)
-        quant_w(0, 2)
-        prep_x(1)
-        quant_x(1)
-        regroup(1)
+        def per_row(values, n):
+            return values[:, 0:rows_of(n)].unsqueeze(2).to_broadcast([P, rows_of(n), 16])
 
-        emit = {
-            "lw": load_w, "lk": load_k, "mm": mm, "e": ev, "rg": regroup, "qw": quant_w_whole,
-            "kt": k_transposes, "ke": k_evac, "qk": quant_k, "qq": quant_q, "qqa": quant_q_a, "qqb": quant_q_b,
-            "s2": s2, "s2b": s2b, "ex": ex,
-        }
+        def row_maxima(n):
+            batch_maxima = soft_pool.tile([P, 24], F32)
+            maxima[n] = batch_maxima
+            nc.vector.tensor_reduce(out=batch_maxima[:, 0:rows_of(n)], in_=by_row(scores[n], n), axis=AX.X, op=ALU.max)
+
+        def subtract_maxima(n, engine):
+            engine.tensor_tensor(out=by_row(scores[n], n), in0=by_row(scores[n], n), in1=per_row(maxima[n], n), op=ALU.subtract)
+
+        def exponentials(n):
+            batch_exps = soft_pool.tile([P, 384], F32)
+            exps[n] = batch_exps
+            width = rows_of(n) * 16
+            nc.scalar.activation(out=batch_exps[:, 0:width], in_=scores[n][:, 0:width], func=ACT.Exp, scale=SCALE)
+
+        def sums_and_reciprocals(n):
+            sums = soft_pool.tile([P, 24], F32)
+            nc.vector.tensor_reduce(out=sums[:, 0:rows_of(n)], in_=by_row(exps[n], n), axis=AX.X, op=ALU.add)
+            batch_reciprocals = soft_pool.tile([P, 24], F32)
+            reciprocals[n] = batch_reciprocals
+            nc.vector.reciprocal(out=batch_reciprocals[:, 0:rows_of(n)], in_=sums[:, 0:rows_of(n)])
+
+        out_rows = out.rearrange("b h (s a) f g -> b (h s) (a f) g", s=3)
+
+        def normalise_and_store(n, engine):
+            h0, h1 = BATCHES[n]
+            engine.tensor_tensor(out=by_row(exps[n], n), in0=by_row(exps[n], n), in1=per_row(reciprocals[n], n), op=ALU.mult)
+            by_clip = exps[n][:, 0:rows_of(n) * 16].rearrange("p (b t g) -> p b t g", b=2, g=16)
+            for b in range(2):
+                nc.sync.dma_start(out=out_rows[b, h0 * 3:h1 * 3].rearrange("t p g -> p t g"), in_=by_clip[:, b])
+
+        transpose_x(0)
+        quantise_x(0)
+        regroup_w(0)
+        quantise_w(0, 2)
+        transpose_x(1)
+        quantise_x(1)
+        regroup_w(1)
+
+        ending_with = {}
+        for n in range(len(BATCHES)):
+            ending_with[BATCHES[n][1] - 1] = n
         for h in range(HEADS):
-            steps = FIRST_STEPS if h == 0 else LAST_STEPS if h == LAST else STEADY_STEPS
-            for step in steps:
-                if step[0] == "sm":
-                    softmax_stage(step[1])
-                elif 0 <= h + step[1] < HEADS:
-                    emit[step[0]](h + step[1], *step[2:])
+            new_q(h)
+            if 0 < h < LAST:
+                quantise_w(h + 1, 1)
+            if h + 4 < HEADS:
+                load_w(h + 4)
+            if h + 2 < HEADS:
+                load_k(h + 2)
+            project(h, 0)
+            round_q(h, 0)
+            project(h, 1)
+            round_q(h, 1)
+            if h + 2 < HEADS:
+                regroup_w(h + 2)
+            project(h, 2)
+            round_q(h, 2)
+            if h - 4 in ending_with:
+                sums_and_reciprocals(ending_with[h - 4])
+            project(h, 3)
+            project(h, 4)
+            if h > 0:
+                multiply_qk(h - 1)
+                extract(h - 1, 0)
+            if h - 2 in ending_with:
+                row_maxima(ending_with[h - 2])
+            if h - 4 in ending_with:
+                normalise_and_store(ending_with[h - 4], nc.gpsimd)
+            round_q(h, 3)
+            if h == 0:
+                quantise_w(1, 1)
+            if h - 3 in ending_with:
+                exponentials(ending_with[h - 3])
+            project(h, 5)
+            transpose_k(h)
+            round_q(h, 4)
+            round_q(h, 5)
+            if h > 0:
+                extract(h - 1, 1)
+            quantise(q_grouped[h], q_mx[h], 0, 2048)
+            if h - 2 in ending_with:
+                subtract_maxima(ending_with[h - 2], nc.gpsimd)
+            quantise(q_grouped[h], q_mx[h], 2048, 1024)
+            regroup_k(h)
+            quantise_k(h)
+
+        multiply_qk(LAST)
+        row_maxima(2)
+        subtract_maxima(2, nc.gpsimd)
+        extract(LAST, 0)
+        extract(LAST, 1)
+        exponentials(2)
+        row_maxima(3)
+        subtract_maxima(3, nc.vector)
+        sums_and_reciprocals(2)
+        normalise_and_store(2, nc.gpsimd)
+        exponentials(3)
+        sums_and_reciprocals(3)
+        normalise_and_store(3, nc.vector)

from contextlib import ExitStack

import concourse.mybir as mybir
from concourse.masks import make_identity

F32 = mybir.dt.float32
BF16 = mybir.dt.bfloat16
U32 = mybir.dt.uint32
U8 = mybir.dt.uint8
FP8X4 = mybir.dt.float8_e4m3fn_x4
ALU = mybir.AluOpType
ACT = mybir.ActivationFunctionType
AX = mybir.AxisListType

P = 128
HEADS = 12
LAST = HEADS - 1
TILES = 6
FLOPS = 2 * 768 * 1024 * 6144 + 2 * 576 * 16 * 16 * 512
SCALE = 1.0 / 96.0
OFF_BLOCK = 2.0 ** 100
VIA_GPSIMD = (0, 1)
BATCHES = ((0, 4), (4, 8), (8, 11), (11, 12))


def tile_dividedspacetimeattention_pa_kernel(tc, x, Wq, bq, k, out):
    nc = tc.nc
    with ExitStack() as ctx:
        consts = ctx.enter_context(tc.tile_pool(name="consts", bufs=1))
        w_raw_pool = ctx.enter_context(tc.tile_pool(name="w_raw", bufs=4))
        k_raw_pool = ctx.enter_context(tc.tile_pool(name="k_raw", bufs=3))
        w_grouped_pool = ctx.enter_context(tc.tile_pool(name="w_grouped", bufs=2))
        w_mx_pool = ctx.enter_context(tc.tile_pool(name="w_mx", bufs=2))
        k_grouped_pool = ctx.enter_context(tc.tile_pool(name="k_grouped", bufs=2))
        k_mx_pool = ctx.enter_context(tc.tile_pool(name="k_mx", bufs=2))
        q_grouped_pool = ctx.enter_context(tc.tile_pool(name="q_grouped", bufs=2))
        q_mx_pool = ctx.enter_context(tc.tile_pool(name="q_mx", bufs=2))
        y_copy_pool = ctx.enter_context(tc.tile_pool(name="y_copy", bufs=2))
        soft_pool = ctx.enter_context(tc.tile_pool(name="soft", bufs=2))
        y_psum = ctx.enter_context(tc.psum_pool(name="y_psum", bufs=3))
        t_psum = ctx.enter_context(tc.psum_pool(name="t_psum", bufs=3))
        s_psum = ctx.enter_context(tc.psum_pool(name="s_psum", bufs=2))
        ctx.enter_context(tc.manual_schedule())

        w_raw, k_raw, w_grouped, w_mx, k_banks, k_grouped, k_mx = {}, {}, {}, {}, {}, {}, {}
        q_grouped, q_mx, y_banks, score_banks = {}, {}, {}, {}
        scores, exps, maxima, reciprocals = {}, {}, {}, {}

        def quantise(src, mx_pair, first, width):
            words, scale_bytes = mx_pair
            nc.vector.quantize_mx(
                out=words[:, first // 4:(first + width) // 4].bitcast(FP8X4),
                scales=scale_bytes[:, first // 4:(first + width) // 4],
                in_=src[:, first:first + width],
            )

        def mx_pass(dst, stationary, m0, moving, n0, start, stop):
            nc.tensor.matmul_mx(
                out=dst,
                lhsT=stationary[0][:, m0:m0 + P].bitcast(FP8X4),
                lhsT_scale=stationary[1][:, m0:m0 + P],
                rhs=moving[0][:, n0:n0 + P].bitcast(FP8X4),
                rhs_scale=moving[1][:, n0:n0 + P],
                start=start,
                stop=stop,
            )

        def load_w(h):
            raw = w_raw_pool.tile([P, 4096], BF16)
            rows = raw[:].rearrange("p (c j w) -> p c j w", c=2, j=4)
            for c in range(2):
                for u in range(2):
                    r0 = 512 * c + 256 * u
                    nc.sync.dma_start(
                        out=rows[:, c, 2 * u:2 * u + 2, :],
                        in_=Wq[r0:r0 + 256, h * 512:(h + 1) * 512].rearrange("(p e) w -> p e w", e=2),
                    )
            w_raw[h] = raw

        k_rows = k.rearrange("b h n g d -> b h (n g) d")

        def load_k(h):
            raw = k_raw_pool.tile([P, 3072], BF16)
            tiles = raw[:].rearrange("p (i d) -> p i d", i=TILES)
            for b in range(2):
                nc.sync.dma_start(
                    out=tiles[:, 3 * b:3 * b + 3, :],
                    in_=k_rows[b, h].rearrange("(s p) d -> p s d", s=3),
                )
            k_raw[h] = raw

        x_raw = consts.tile([P, 6144], BF16)

        def load_x(b):
            nc.sync.dma_start(
                out=x_raw[:].rearrange("p (b r c) -> p b r c", b=2, r=3)[:, b],
                in_=x[b].rearrange("(p r) c -> p r c", r=3),
            )

        identity = consts.tile([P, P], F32)
        make_identity(nc, identity[:])
        table_warmer = consts.tile([P, 2], F32)
        nc.vector.memset(table_warmer[:], 0.0)
        nc.scalar.activation(out=table_warmer[:, 1:2], in_=table_warmer[:, 0:1], func=ACT.Exp)
        bias_rows = consts.tile([P, 256], BF16)
        nc.vector.memset(bias_rows[:], 0.0)
        mask_values = consts.tile([P, 1024], BF16, align_bytes=64)
        nc.vector.memset(mask_values[:], 0.0)

        load_x(0)
        nc.sync.dma_start(out=bias_rows[0:24, :], in_=bq.rearrange("(r c) -> r c", c=256))
        load_w(0)
        load_x(1)
        load_w(1)
        load_w(2)
        load_k(0)
        load_w(3)
        load_k(1)

        mask_slots = mask_values[:].rearrange("p (o a f j) -> p o a f j", o=2, a=8, f=16)
        same_patch = identity[:, 0:8].unsqueeze(2).to_broadcast([P, 8, 16])
        nc.vector.tensor_copy(out=mask_slots[:, 0, :, :, 0], in_=same_patch)
        nc.vector.tensor_scalar(
            out=mask_slots[:, 1, :, :, 0], in0=same_patch, scalar1=-1.0, scalar2=OFF_BLOCK, op0=ALU.add, op1=ALU.mult
        )
        mask_words = consts.tile([P, 256], U32, align_bytes=64)
        mask_scales = consts.tile([P, 256], U8, align_bytes=64)
        mask_mx = (mask_words, mask_scales)
        quantise(mask_values, mask_mx, 0, 1024)

        bias_bank = t_psum.tile([P, 512], F32, tag="t")
        nc.tensor.transpose(bias_bank[:, 0:P], bias_rows[:].bitcast(F32), identity[:])
        bias = consts.tile([P, 48], F32)
        nc.vector.tensor_copy(out=bias[:], in_=bias_bank[:, 0:24].bitcast(BF16))

        x_words = x_raw[:].bitcast(F32).rearrange("p (b r w) -> p b r w", b=2, r=3)
        x_grouped = consts.tile([P, 6144], BF16, align_bytes=64)
        x_grouped_words = x_grouped[:].bitcast(F32).rearrange("p (c n f u) -> p c n f u", c=2, n=48, f=16)
        x_codes = consts.tile([P, 1536], U32, align_bytes=64)
        x_scales = consts.tile([P, 1536], U8, align_bytes=64)
        x_mx = (x_codes, x_scales)

        def transpose_x(b):
            for r in range(3):
                bank = t_psum.tile([P, 512], F32, tag="t")
                halves = bank[:].rearrange("p (q t) -> p q t", q=4)
                for q in range(4):
                    nc.tensor.transpose(halves[:, q, :], x_words[:, b, r, q * P:(q + 1) * P], identity[:])
                for c in range(2):
                    dst = x_grouped_words[:, c, b * 24 + r:(b + 1) * 24:3, :, :]
                    src = halves[:, 2 * c:2 * c + 2, :].rearrange("p u (f a) -> p a f u", a=8)
                    if c == 0:
                        nc.vector.tensor_copy(out=dst, in_=src)
                    else:
                        nc.scalar.copy(out=dst, in_=src)

        def quantise_x(b):
            for c in range(2):
                quantise(x_grouped, x_mx, c * 3072 + b * 1536, 1024)
                quantise(x_grouped, x_mx, c * 3072 + b * 1536 + 1024, 512)

        def regroup_w(h):
            grouped = w_grouped_pool.tile([P, 4096], BF16, align_bytes=64)
            dst = grouped[:].rearrange("p (c e v i j) -> p c e v j i", c=2, e=2, v=64, i=4, j=4)
            src = w_raw[h][:].rearrange("p (c j v i e) -> p c e v j i", c=2, j=4, v=64, i=4, e=2)
            for c in range(2):
                for e in range(2):
                    if h == 0 and e == 0:
                        nc.vector.tensor_copy(out=dst[:, c, e], in_=src[:, c, e])
                    elif h > 0 and c == 1 and e == 1:
                        nc.gpsimd.tensor_scalar(
                            out=dst[:, c, e], in0=src[:, c, e], scalar1=1.0, scalar2=0.0, op0=ALU.mult, op1=ALU.add
                        )
                    else:
                        nc.scalar.copy(out=dst[:, c, e], in_=src[:, c, e])
            w_grouped[h] = grouped

        def quantise_w(h, calls):
            words = w_mx_pool.tile([P, 1024], U32, align_bytes=64)
            scale_bytes = w_mx_pool.tile([P, 1024], U8, align_bytes=64)
            w_mx[h] = (words, scale_bytes)
            for n in range(calls):
                quantise(w_grouped[h], w_mx[h], n * (4096 // calls), 4096 // calls)

        def transpose_k(h):
            words = k_raw[h][:].bitcast(F32).rearrange("p (i w) -> p i w", i=TILES)
            k_banks[h] = []
            for pair in range(3):
                bank = t_psum.tile([P, 512], F32, tag="t")
                halves = bank[:].rearrange("p (i u r) -> p i u r", i=2, u=2)
                for i in range(2):
                    for u in range(2):
                        nc.tensor.transpose(halves[:, i, u, :], words[:, 2 * pair + i, u * P:(u + 1) * P], identity[:])
                k_banks[h].append(halves)

        def regroup_k(h):
            grouped = k_grouped_pool.tile([P, 3072], BF16, align_bytes=64)
            grouped_words = grouped[:].bitcast(F32).rearrange("p (i r u) -> p i r u", i=TILES, u=2)
            for pair in range(3):
                nc.scalar.copy(
                    out=grouped_words[:, 2 * pair:2 * pair + 2], in_=k_banks[h][pair].rearrange("p i u r -> p i r u")
                )
            k_grouped[h] = grouped

        def quantise_k(h):
            words = k_mx_pool.tile([P, 768], U32, align_bytes=64)
            scale_bytes = k_mx_pool.tile([P, 768], U8, align_bytes=64)
            k_mx[h] = (words, scale_bytes)
            quantise(k_grouped[h], k_mx[h], 0, 2048)
            quantise(k_grouped[h], k_mx[h], 2048, 1024)

        def project(h, i):
            bank = y_psum.tile([P, 512], F32, tag="y")
            slots = bank[:].rearrange("p (j r) -> p j r", j=4)
            for j in range(4):
                output_tile = 2 * (j % 2) + j // 2
                for c in range(2):
                    mx_pass(slots[:, j, :], w_mx[h], c * 512 + output_tile * P, x_mx, c * 768 + i * P, c == 0, c == 1)
            y_banks[(h, i)] = bank

        def new_q(h):
            grouped = q_grouped_pool.tile([P, 3072], BF16, align_bytes=64)
            words = q_mx_pool.tile([P, 768], U32, align_bytes=64)
            scale_bytes = q_mx_pool.tile([P, 768], U8, align_bytes=64)
            q_grouped[h] = grouped
            q_mx[h] = (words, scale_bytes)

        def round_q(h, i):
            y_by_token = y_banks[(h, i)][:].rearrange("p (j r) -> p r j", j=4)
            q_by_token = q_grouped[h][:, i * 512:(i + 1) * 512].rearrange("p (r j) -> p r j", j=4)
            bias_by_token = bias[:, h * 4:(h + 1) * 4].unsqueeze(1).to_broadcast([P, P, 4])
            if h > 0 and i in VIA_GPSIMD:
                y_copy = y_copy_pool.tile([P, 512], F32)
                y_copy_by_token = y_copy[:].rearrange("p (r j) -> p r j", j=4)
                nc.scalar.copy(out=y_copy_by_token, in_=y_by_token)
                nc.gpsimd.tensor_tensor(out=q_by_token, in0=y_copy_by_token, in1=bias_by_token, op=ALU.add)
            else:
                nc.vector.tensor_tensor(out=q_by_token, in0=y_by_token, in1=bias_by_token, op=ALU.add)

        def multiply_qk(h):
            for b in range(2):
                bank = s_psum.tile([P, 384], F32, tag="s")
                tiles = bank[:].rearrange("p (s c) -> p s c", s=3)
                for s in range(3):
                    i = 3 * b + s
                    mx_pass(tiles[:, s, :], q_mx[h], i * P, k_mx[h], i * P, True, False)
                    mx_pass(tiles[:, s, :], mask_mx, 0, mask_mx, P, False, True)
                score_banks[(h, b)] = bank

        def batch_of(h):
            return [n for n in range(len(BATCHES)) if BATCHES[n][0] <= h < BATCHES[n][1]][0]

        def extract(h, b):
            n = batch_of(h)
            h0, h1 = BATCHES[n]
            if n not in scores:
                batch_scores = soft_pool.tile([P, 384], F32)
                scores[n] = batch_scores
            first = (b * (h1 - h0) + h - h0) * 48
            nc.vector.tensor_reduce(
                out=scores[n][:, first:first + 48].rearrange("p (s g) -> p s g", g=16),
                in_=score_banks[(h, b)][:].rearrange("p (s a g) -> p s g a", s=3, a=8),
                axis=AX.X,
                op=ALU.max,
            )

        def rows_of(n):
            return (BATCHES[n][1] - BATCHES[n][0]) * TILES

        def by_row(tile_of_batch, n):
            return tile_of_batch[:, 0:rows_of(n) * 16].rearrange("p (t g) -> p t g", g=16)

        def per_row(values, n):
            return values[:, 0:rows_of(n)].unsqueeze(2).to_broadcast([P, rows_of(n), 16])

        def row_maxima(n):
            batch_maxima = soft_pool.tile([P, 24], F32)
            maxima[n] = batch_maxima
            nc.vector.tensor_reduce(out=batch_maxima[:, 0:rows_of(n)], in_=by_row(scores[n], n), axis=AX.X, op=ALU.max)

        def subtract_maxima(n, engine):
            engine.tensor_tensor(out=by_row(scores[n], n), in0=by_row(scores[n], n), in1=per_row(maxima[n], n), op=ALU.subtract)

        def exponentials(n):
            batch_exps = soft_pool.tile([P, 384], F32)
            exps[n] = batch_exps
            width = rows_of(n) * 16
            nc.scalar.activation(out=batch_exps[:, 0:width], in_=scores[n][:, 0:width], func=ACT.Exp, scale=SCALE)

        def sums_and_reciprocals(n):
            sums = soft_pool.tile([P, 24], F32)
            nc.vector.tensor_reduce(out=sums[:, 0:rows_of(n)], in_=by_row(exps[n], n), axis=AX.X, op=ALU.add)
            batch_reciprocals = soft_pool.tile([P, 24], F32)
            reciprocals[n] = batch_reciprocals
            nc.vector.reciprocal(out=batch_reciprocals[:, 0:rows_of(n)], in_=sums[:, 0:rows_of(n)])

        out_rows = out.rearrange("b h (s a) f g -> b (h s) (a f) g", s=3)

        def normalise_and_store(n, engine):
            h0, h1 = BATCHES[n]
            engine.tensor_tensor(out=by_row(exps[n], n), in0=by_row(exps[n], n), in1=per_row(reciprocals[n], n), op=ALU.mult)
            by_clip = exps[n][:, 0:rows_of(n) * 16].rearrange("p (b t g) -> p b t g", b=2, g=16)
            for b in range(2):
                nc.sync.dma_start(out=out_rows[b, h0 * 3:h1 * 3].rearrange("t p g -> p t g"), in_=by_clip[:, b])

        transpose_x(0)
        quantise_x(0)
        regroup_w(0)
        quantise_w(0, 2)
        transpose_x(1)
        quantise_x(1)
        regroup_w(1)

        ending_with = {}
        for n in range(len(BATCHES)):
            ending_with[BATCHES[n][1] - 1] = n
        for h in range(HEADS):
            new_q(h)
            if 0 < h < LAST:
                quantise_w(h + 1, 1)
            if h + 4 < HEADS:
                load_w(h + 4)
            if h + 2 < HEADS:
                load_k(h + 2)
            project(h, 0)
            round_q(h, 0)
            project(h, 1)
            round_q(h, 1)
            if h + 2 < HEADS:
                regroup_w(h + 2)
            project(h, 2)
            round_q(h, 2)
            if h - 4 in ending_with:
                sums_and_reciprocals(ending_with[h - 4])
            project(h, 3)
            project(h, 4)
            if h > 0:
                multiply_qk(h - 1)
                extract(h - 1, 0)
            if h - 2 in ending_with:
                row_maxima(ending_with[h - 2])
            if h - 4 in ending_with:
                normalise_and_store(ending_with[h - 4], nc.gpsimd)
            round_q(h, 3)
            if h == 0:
                quantise_w(1, 1)
            if h - 3 in ending_with:
                exponentials(ending_with[h - 3])
            project(h, 5)
            transpose_k(h)
            round_q(h, 4)
            round_q(h, 5)
            if h > 0:
                extract(h - 1, 1)
            quantise(q_grouped[h], q_mx[h], 0, 2048)
            if h - 2 in ending_with:
                subtract_maxima(ending_with[h - 2], nc.gpsimd)
            quantise(q_grouped[h], q_mx[h], 2048, 1024)
            regroup_k(h)
            quantise_k(h)

        multiply_qk(LAST)
        row_maxima(2)
        subtract_maxima(2, nc.gpsimd)
        extract(LAST, 0)
        extract(LAST, 1)
        exponentials(2)
        row_maxima(3)
        subtract_maxima(3, nc.vector)
        sums_and_reciprocals(2)
        normalise_and_store(2, nc.gpsimd)
        exponentials(3)
        sums_and_reciprocals(3)
        normalise_and_store(3, nc.vector)
